import numpy as np
import ml_dtypes


def mxq(x, axis, fmt="e4m3"):
    dtype, down = {"e4m3": (ml_dtypes.float8_e4m3fn, 7), "e5m2": (ml_dtypes.float8_e5m2, 14)}[fmt]
    v = np.moveaxis(np.asarray(x, np.float32).astype(ml_dtypes.bfloat16).astype(np.float64), axis, -1)
    blocks = v.reshape(v.shape[:-1] + (-1, 32))
    amax = np.abs(blocks).max(-1, keepdims=True)
    byte = np.maximum(np.where(amax > 0, np.frexp(amax)[1] - 1 + 127, 0) - down, 1)
    scale = np.exp2(byte - 127.0)
    codes = (blocks / scale).astype(np.float32).astype(dtype).astype(np.float64)
    return np.moveaxis((codes * scale).reshape(v.shape), -1, axis)


WIDE = False


def mx_kscale(k):
    if not WIDE:
        return np.ones(k)
    levels = np.array([10, -10, 5, -5, 0])
    a = np.random.permutation(np.resize(levels, k // 512 * 4)).reshape(k // 512, 4)
    idx = np.arange(k)
    return np.exp2(a[idx // 512, idx % 128 // 32])


BF16 = ml_dtypes.bfloat16


def bf(x):
    return np.asarray(x, np.float32).astype(BF16)


def f64(x):
    return np.asarray(x).astype(np.float64)


E2M1 = np.array([0.0, 0.5, 1.0, 1.5, 2.0, 3.0, 4.0, 6.0, -0.0, -0.5, -1.0, -1.5, -2.0, -3.0, -4.0, -6.0])


def pack_weight(w, fmt):
    k, n = w.shape
    w = f64(bf(w)).reshape(k // 32, 32, n)
    amax = np.abs(w).max(1)
    if fmt == "e4m3":
        byte = np.frexp(amax)[1] - 1 + 127 - 7
    else:
        mant, ex = np.frexp(amax / 6.0)
        byte = np.where(mant > 0.5, ex, ex - 1) + 127
    byte = np.clip(np.where(amax > 0, byte, 1), 1, 254)
    scaled = (w * np.exp2(127.0 - byte)[:, None, :]).reshape(k, n).astype(np.float32)
    by_word = np.ascontiguousarray(scaled.reshape(k // 512, 128, 4, n).transpose(0, 1, 3, 2))
    if fmt == "e4m3":
        words = by_word.astype(ml_dtypes.float8_e4m3fn).view(np.uint8)
    else:
        c = by_word.astype(ml_dtypes.float4_e2m1fn).view(np.uint8) & 0xF
        words = c[..., 0::2] | (c[..., 1::2] << 4)
    return np.ascontiguousarray(words), np.ascontiguousarray(byte.astype(np.uint8).reshape(k // 512, 16, n))


def unpack_weight(words, scales, fmt):
    g, p, n, _ = words.shape
    if fmt == "e4m3":
        vals = np.ascontiguousarray(words).view(ml_dtypes.float8_e4m3fn).astype(np.float64)
    else:
        nib = np.empty((g, p, n, 4), np.uint8)
        nib[..., 0::2] = words & 0xF
        nib[..., 1::2] = words >> 4
        vals = E2M1[nib]
    vals = vals * np.repeat(np.exp2(scales.astype(np.float64) - 127.0), 8, axis=1)[..., None]
    return vals.transpose(0, 1, 3, 2).reshape(g * 512, n)


B, DIM, HID, H, SEQ, DOUT = 512, 2048, 256, 8, 2048, 2048
DECAY_CONSTANT = SEQ // 512
H2 = H // 2
F = H * HID


def setup_inputs():
    s = mx_kscale(DIM)
    x = bf(np.random.standard_normal((B, DIM)) * s)
    W_proj = bf(np.random.standard_normal((H, DIM, HID)) / np.sqrt(DIM) / s[:, None])
    b_proj = bf(np.random.standard_normal((H, HID)) * 0.1)
    W_out_words, W_out_scales = pack_weight(np.random.standard_normal((F, DOUT)) / np.sqrt(F), "e4m3")
    b_out = bf(np.random.standard_normal(DOUT) * 0.1)
    w_mix = bf(np.concatenate([0.4 + 0.05 * np.random.standard_normal((H2, SEQ)), -0.3 + 0.05 * np.random.standard_normal((H - H2, SEQ))], axis=0))
    b_mix = bf(np.concatenate([3.0 + 0.1 * np.random.standard_normal((H2, SEQ)), 0.2 + 0.1 * np.random.standard_normal((H - H2, SEQ))], axis=0))
    decay_values = bf(0.95 + 0.05 * np.random.standard_normal(H))
    caches = bf(np.random.standard_normal((H, B, HID)))
    return {"x": x, "index": 7, "W_proj": W_proj, "b_proj": b_proj, "W_out_words": W_out_words, "W_out_scales": W_out_scales, "b_out": b_out,
            "w_mix": w_mix, "b_mix": b_mix, "decay_values": decay_values, "caches": caches}


def reference(x, index, W_proj, b_proj, W_out_words, W_out_scales, b_out, w_mix, b_mix, decay_values, caches):
    proj = (mxq(f64(x), 1, "e4m3") @ mxq(f64(W_proj), 1, "e4m3")) + f64(b_proj)[:, None, :]
    decay = np.clip(f64(decay_values), 0.9, 1.0) ** (1.0 / DECAY_CONSTANT)
    w = f64(w_mix)[:, index]
    b = f64(b_mix)[:, index]
    cache_coef = np.concatenate([w[:H2] * decay[:H2], decay[H2:]], axis=0)
    out = (w[:, None, None] * proj
           + cache_coef[:, None, None] * f64(caches)
           + b[:, None, None])
    hidden = np.transpose(out, (1, 0, 2)).reshape(B, H * HID)
    return (mxq(hidden, 1, "e4m3") @ unpack_weight(W_out_words, W_out_scales, "e4m3")) + f64(b_out)

@@ -1,0 +1,257 @@
+from contextlib import ExitStack
+
+import concourse.mybir as mybir
+from concourse.masks import make_identity
+
+F32 = mybir.dt.float32
+BF16 = mybir.dt.bfloat16
+U32 = mybir.dt.uint32
+U8 = mybir.dt.uint8
+I32 = mybir.dt.int32
+FP8X4 = mybir.dt.float8_e4m3fn_x4
+ALU = mybir.AluOpType
+ACT = mybir.ActivationFunctionType
+
+P = 128
+PACK = 4
+K_PASS = P * PACK
+BATCH, DIM, HID, HEADS, DOUT = 512, 2048, 256, 8, 2048
+BATCH_TILES = BATCH // P
+PASSES = DIM // K_PASS
+HALVES = PASSES // 2
+GROUPS = HEADS * HID // K_PASS
+GROUP_HEADS = HEADS // GROUPS
+HEAD_PARTS = HID // PACK
+N_TILE = 512
+OUT_TILES = DOUT // N_TILE
+WORDS = K_PASS // 2
+SLOT = 16
+HEAD_COLS = 64
+W_ROW, B_ROW, COEF_ROW = 0, 1, 2
+
+FLOPS = 2 * BATCH * DIM * HEADS * HID + 2 * BATCH * HEADS * HID * DOUT
+
+
+def tile_mixedrepeatheads_kernel(
+    tc, x, index, W_proj, b_proj, W_out_words, W_out_scales, b_out, w_mix, b_mix, decay_values, caches, out
+):
+    nc = tc.nc
+    decay_root = 1.0 / (w_mix.shape[1] // 512)
+    x_rows = x.rearrange("(p i) k -> p i k", i=BATCH_TILES)
+    out_rows = out.rearrange("(p i) n -> p i n", i=BATCH_TILES)
+
+    with ExitStack() as ctx:
+        const = ctx.enter_context(tc.tile_pool(name="const", bufs=1))
+        keep = ctx.enter_context(tc.tile_pool(name="keep", bufs=1))
+        ring = ctx.enter_context(tc.tile_pool(name="ring", bufs=GROUPS * HALVES))
+        pair = ctx.enter_context(tc.tile_pool(name="pair", bufs=2))
+        triple = ctx.enter_context(tc.tile_pool(name="triple", bufs=3))
+        store_pool = ctx.enter_context(tc.tile_pool(name="store", bufs=4))
+        psum = ctx.enter_context(tc.psum_pool(name="psum", bufs=8))
+
+        def load_half_group(g, half):
+            raw = ring.tile([P, GROUP_HEADS, 2, PACK, HID], BF16, name="raw", tag="weights", align_bytes=64)
+            for hh in range(GROUP_HEADS):
+                by_pass = W_proj[GROUP_HEADS * g + hh].rearrange("(c q j) n -> q c j n", c=PASSES, j=PACK)
+                nc.sync.dma_start(out=raw[:, hh], in_=by_pass[:, 2 * half : 2 * half + 2])
+            return raw
+
+        def load_caches(g):
+            cache_sb = keep.tile([P, BATCH_TILES, GROUP_HEADS, HID], BF16, name="cache_sb%d" % g)
+            for hh in range(GROUP_HEADS):
+                nc.sync.dma_start(
+                    out=cache_sb[:, :, hh, :],
+                    in_=caches[GROUP_HEADS * g + hh].rearrange("(p i) n -> p i n", i=BATCH_TILES),
+                )
+            return cache_sb
+
+        w_raw = {(0, half): load_half_group(0, half) for half in range(HALVES)}
+        x_sb = keep.tile([P, BATCH_TILES, DIM], BF16)
+        for i in range(BATCH_TILES):
+            nc.sync.dma_start(out=x_sb[:, i, :], in_=x_rows[:, i, :])
+        cache_tiles = [load_caches(0)]
+        for g in range(1, GROUPS):
+            for half in range(HALVES):
+                w_raw[(g, half)] = load_half_group(g, half)
+            cache_tiles.append(load_caches(g))
+
+        out_scales = keep.tile([P, DOUT], U8, align_bytes=64)
+        nc.vector.memset(out_scales[:].bitcast(I32), 0)
+        for quadrant in range(4):
+            nc.sync.dma_start(
+                out=out_scales[32 * quadrant : 32 * quadrant + 4 * GROUPS, :].bitcast(I32),
+                in_=W_out_scales[:, 4 * quadrant : 4 * quadrant + 4, :].bitcast(I32),
+            )
+        word_bytes = W_out_words.rearrange("g q n t -> q g (n t)")
+        out_words = []
+        for n in range(OUT_TILES):
+            words = ring.tile([P, GROUPS, N_TILE], U32, name="words", tag="weights", align_bytes=64)
+            nc.sync.dma_start(
+                out=words[:].bitcast(I32), in_=word_bytes[:, :, PACK * n * N_TILE : PACK * (n + 1) * N_TILE].bitcast(I32)
+            )
+            out_words.append(words)
+
+        ident = const.tile([P, P], F32)
+        make_identity(nc, ident[:])
+        ones = const.tile([P, P], BF16)
+        nc.vector.memset(ones[:], 1.0)
+        rows = const.tile([P, DOUT + HEAD_COLS], BF16)
+        nc.vector.memset(rows[:].bitcast(I32), 0)
+        nc.scalar.dma_start(out=rows[0:1, 0:DOUT], in_=b_out.unsqueeze(0))
+        with nc.allow_non_contiguous_dma(reason="one element of each head's row"):
+            for row, table in ((W_ROW, w_mix), (B_ROW, b_mix)):
+                nc.scalar.dma_start(
+                    out=rows[0:1, DOUT + SLOT * row : DOUT + SLOT * row + HEADS],
+                    in_=table[:, index : index + 1].rearrange("h o -> o h"),
+                )
+        nc.scalar.dma_start(
+            out=rows[0:1, DOUT + SLOT * COEF_ROW : DOUT + SLOT * COEF_ROW + HEADS], in_=decay_values.unsqueeze(0)
+        )
+        proj_bias = const.tile([P, GROUPS, PACK], BF16)
+        nc.scalar.dma_start(
+            out=proj_bias[:], in_=b_proj.rearrange("h c -> (h c)").rearrange("(g q t) -> q g t", g=GROUPS, t=PACK)
+        )
+
+        out_bias = const.tile([P, DOUT], F32)
+        for n in range(OUT_TILES):
+            n_cols = slice(n * N_TILE, (n + 1) * N_TILE)
+            spread = psum.tile([P, N_TILE], F32, tag="bank")
+            nc.tensor.matmul(out=spread[:], lhsT=ones[:], rhs=rows[:, n_cols], start=True, stop=True)
+            nc.scalar.copy(out=out_bias[:, n_cols], in_=spread[:])
+        spread_heads = psum.tile([P, HEAD_COLS], F32, tag="bank")
+        nc.tensor.matmul(
+            out=spread_heads[:], lhsT=ones[:], rhs=rows[:, DOUT : DOUT + HEAD_COLS], start=True, stop=True
+        )
+        per_head = const.tile([P, 3, HEADS], F32)
+        nc.vector.tensor_copy(
+            out=per_head[:], in_=spread_heads[:].rearrange("p (r s) -> p r s", s=SLOT)[:, 0:3, 0:HEADS]
+        )
+        nc.vector.tensor_scalar(
+            out=per_head[:, COEF_ROW, :], in0=per_head[:, COEF_ROW, :],
+            scalar1=0.9, scalar2=1.0, op0=ALU.max, op1=ALU.min,
+        )
+        exponent = const.tile([P, HEADS], F32)
+        nc.vector.memset(exponent[:], decay_root)
+        nc.gpsimd.tensor_tensor(
+            out=per_head[:, COEF_ROW, :], in0=per_head[:, COEF_ROW, :], in1=exponent[:], op=ALU.pow
+        )
+        first_heads = slice(0, HEADS // 2)
+        nc.vector.tensor_tensor(
+            out=per_head[:, COEF_ROW, first_heads], in0=per_head[:, COEF_ROW, first_heads],
+            in1=per_head[:, W_ROW, first_heads], op=ALU.mult,
+        )
+        per_part = const.tile([P, 3, GROUPS], F32)
+        for hh in range(GROUP_HEADS):
+            parts = slice(hh * HEAD_PARTS, (hh + 1) * HEAD_PARTS)
+            nc.vector.tensor_copy(out=per_part[parts], in_=per_head[parts, :, hh:HEADS:GROUP_HEADS])
+        shift = const.tile([P, GROUPS, PACK], F32)
+        for g in range(GROUPS):
+            nc.vector.tensor_scalar(
+                out=shift[:, g, :], in0=proj_bias[:, g, :],
+                scalar1=per_part[:, W_ROW, g : g + 1], scalar2=per_part[:, B_ROW, g : g + 1],
+                op0=ALU.mult, op1=ALU.add,
+            )
+
+        def quantise_weights(g):
+            w_codes = pair.tile([P, PASSES, PACK, P], U32, name="w_codes", align_bytes=64)
+            w_scales = pair.tile([P, PASSES, PACK, P], U8, name="w_scales", align_bytes=64)
+            for half in range(HALVES):
+                w_grouped = triple.tile([P, 2, PACK, P, PACK], BF16, name="w_grouped", align_bytes=64)
+                for hh in range(GROUP_HEADS):
+                    parts = slice(hh * HEAD_PARTS, (hh + 1) * HEAD_PARTS)
+                    for cc in range(2):
+                        sorted_view = w_grouped[:, cc, :, parts, :].rearrange("q t m j -> q m j t")
+                        raw_view = w_raw[(g, half)][:, hh, cc].rearrange("q j (m t) -> q m j t", t=PACK)
+                        if cc == 0:
+                            nc.vector.tensor_copy(out=sorted_view, in_=raw_view)
+                        else:
+                            nc.scalar.copy(out=sorted_view, in_=raw_view)
+                two = slice(2 * half, 2 * half + 2)
+                nc.vector.quantize_mx(
+                    out=w_codes[:, two].rearrange("q c t m -> q (c t m)").bitcast(FP8X4),
+                    scales=w_scales[:, two].rearrange("q c t m -> q (c t m)"),
+                    in_=w_grouped[:].rearrange("q c t m j -> q (c t m j)"),
+                )
+            return w_codes, w_scales
+
+        first_weights = quantise_weights(0)
+
+        x_codes = keep.tile([P, BATCH_TILES, PASSES, P], U32, align_bytes=64)
+        x_scales = keep.tile([P, BATCH_TILES, PASSES, P], U8, align_bytes=64)
+        for i in range(BATCH_TILES):
+            x_words = x_sb[:, i, :].bitcast(F32)
+            x_grouped = pair.tile([P, PASSES, P, PACK], BF16, align_bytes=64)
+            for half in range(HALVES):
+                x_t = psum.tile([P, 2, 2, P], F32, tag="bank")
+                for cc in range(2):
+                    first = WORDS * (2 * half + cc)
+                    for u in range(2):
+                        nc.tensor.transpose(x_t[:, cc, u, :], x_words[:, first + u : first + WORDS : 2], ident[:])
+                nc.scalar.copy(
+                    out=x_grouped[:, 2 * half : 2 * half + 2].bitcast(F32), in_=x_t[:].rearrange("q c u p -> q c p u")
+                )
+            nc.vector.quantize_mx(
+                out=x_codes[:, i].rearrange("q c p -> q (c p)").bitcast(FP8X4),
+                scales=x_scales[:, i].rearrange("q c p -> q (c p)"),
+                in_=x_grouped[:].rearrange("q c p t -> q (c p t)"),
+            )
+
+        hid_codes = keep.tile([P, GROUPS, BATCH], U32, align_bytes=64)
+        hid_scales = keep.tile([P, GROUPS, BATCH], U8, align_bytes=64)
+
+        for g in range(GROUPS):
+            w_codes, w_scales = first_weights if g == 0 else quantise_weights(g)
+
+            rest = pair.tile([P, PACK, BATCH_TILES, P], F32)
+            for u in range(2):
+                cache_t = psum.tile([P, BATCH_TILES, P], F32, tag="bank")
+                for i in range(BATCH_TILES):
+                    cache_words = cache_tiles[g][:, i].rearrange("p h n -> p (h n)").bitcast(F32)
+                    nc.tensor.transpose(cache_t[:, i, :], cache_words[:, u:WORDS:2], ident[:])
+                halves = cache_t[:].bitcast(BF16).rearrange("q i (p e) -> q i p e", e=2)
+                for e in range(2):
+                    t = 2 * u + e
+                    nc.scalar.activation(
+                        out=rest[:, t], in_=halves[:, :, :, e], func=ACT.Identity,
+                        scale=per_part[:, COEF_ROW, g : g + 1], bias=shift[:, g, t : t + 1],
+                    )
+
+            hid_grouped = pair.tile([P, BATCH_TILES, P, PACK], BF16, align_bytes=64)
+            for i in range(BATCH_TILES):
+                proj = psum.tile([P, PACK, P], F32, tag="bank")
+                for t in range(PACK):
+                    for c in range(PASSES):
+                        nc.tensor.matmul_mx(
+                            out=proj[:, t, :],
+                            lhsT=w_codes[:, c, t, :].bitcast(FP8X4), lhsT_scale=w_scales[:, c, t, :],
+                            rhs=x_codes[:, i, c, :].bitcast(FP8X4), rhs_scale=x_scales[:, i, c, :],
+                            start=(c == 0), stop=(c == PASSES - 1),
+                        )
+                nc.vector.scalar_tensor_tensor(
+                    out=hid_grouped[:, i],
+                    in0=proj[:].rearrange("q t p -> q p t"), scalar=per_part[:, W_ROW, g : g + 1],
+                    in1=rest[:, :, i, :].rearrange("q t p -> q p t"),
+                    op0=ALU.mult, op1=ALU.add,
+                )
+            nc.vector.quantize_mx(
+                out=hid_codes[:, g, :].bitcast(FP8X4), scales=hid_scales[:, g, :],
+                in_=hid_grouped[:].rearrange("q i p t -> q (i p t)"),
+            )
+
+        for n in range(OUT_TILES):
+            n_cols = slice(n * N_TILE, (n + 1) * N_TILE)
+            accs = [psum.tile([P, N_TILE], F32, name="acc", tag="bank") for i in range(BATCH_TILES)]
+            for g in range(GROUPS):
+                for i in range(BATCH_TILES):
+                    nc.tensor.matmul_mx(
+                        out=accs[i][:],
+                        lhsT=hid_codes[:, g, i * P : (i + 1) * P].bitcast(FP8X4),
+                        lhsT_scale=hid_scales[:, g, i * P : (i + 1) * P],
+                        rhs=out_words[n][:, g, :].bitcast(FP8X4),
+                        rhs_scale=out_scales[4 * g : P, n_cols],
+                        start=(g == 0), stop=(g == GROUPS - 1),
+                    )
+            for i in range(BATCH_TILES):
+                result = store_pool.tile([P, N_TILE], F32)
+                nc.vector.tensor_tensor(out=result[:], in0=accs[i][:], in1=out_bias[:, n_cols], op=ALU.add)
+                nc.sync.dma_start(out=out_rows[:, i, n_cols], in_=result[:])

@@ -41,12 +41,13 @@ def tile_mixedrepeatheads_kernel(
     out_rows = out.rearrange("(p i) n -> p i n", i=BATCH_TILES)
 
     with ExitStack() as ctx:
+        ctx.enter_context(tc.manual_schedule())
         const = ctx.enter_context(tc.tile_pool(name="const", bufs=1))
         keep = ctx.enter_context(tc.tile_pool(name="keep", bufs=1))
         ring = ctx.enter_context(tc.tile_pool(name="ring", bufs=GROUPS * HALVES))
         pair = ctx.enter_context(tc.tile_pool(name="pair", bufs=2))
         triple = ctx.enter_context(tc.tile_pool(name="triple", bufs=3))
-        store_pool = ctx.enter_context(tc.tile_pool(name="store", bufs=4))
+        store_pool = ctx.enter_context(tc.tile_pool(name="store", bufs=8))
         psum = ctx.enter_context(tc.psum_pool(name="psum", bufs=8))
 
         def load_half_group(g, half):
@@ -65,15 +66,37 @@ def tile_mixedrepeatheads_kernel(
                 )
             return cache_sb
 
-        w_raw = {(0, half): load_half_group(0, half) for half in range(HALVES)}
+        def load_small_vectors():
+            nc.sync.dma_start(out=rows[0:1, 0:DOUT], in_=b_out.unsqueeze(0))
+            with nc.allow_non_contiguous_dma(reason="one element of each head's row"):
+                for row, table in ((W_ROW, w_mix), (B_ROW, b_mix)):
+                    nc.sync.dma_start(
+                        out=rows[0:1, DOUT + SLOT * row : DOUT + SLOT * row + HEADS],
+                        in_=table[:, index : index + 1].rearrange("h o -> o h"),
+                    )
+            nc.sync.dma_start(
+                out=rows[0:1, DOUT + SLOT * COEF_ROW : DOUT + SLOT * COEF_ROW + HEADS], in_=decay_values.unsqueeze(0)
+            )
+            nc.sync.dma_start(
+                out=proj_bias[:], in_=b_proj.rearrange("h c -> (h c)").rearrange("(g q t) -> q g t", g=GROUPS, t=PACK)
+            )
+
+        rows = const.tile([P, DOUT + HEAD_COLS], BF16)
+        nc.vector.memset(rows[:].bitcast(I32), 0)
+        proj_bias = const.tile([P, GROUPS, PACK], BF16)
+
+        w_raw = {}
+        cache_tiles = []
         x_sb = keep.tile([P, BATCH_TILES, DIM], BF16)
-        for i in range(BATCH_TILES):
-            nc.sync.dma_start(out=x_sb[:, i, :], in_=x_rows[:, i, :])
-        cache_tiles = [load_caches(0)]
-        for g in range(1, GROUPS):
+        for g in range(GROUPS):
             for half in range(HALVES):
                 w_raw[(g, half)] = load_half_group(g, half)
+                if (g, half) == (0, 0):
+                    load_small_vectors()
             cache_tiles.append(load_caches(g))
+            if g == 0:
+                for i in range(BATCH_TILES):
+                    nc.sync.dma_start(out=x_sb[:, i, :], in_=x_rows[:, i, :])
 
         out_scales = keep.tile([P, DOUT], U8, align_bytes=64)
         nc.vector.memset(out_scales[:].bitcast(I32), 0)
@@ -95,163 +118,221 @@ def tile_mixedrepeatheads_kernel(
         make_identity(nc, ident[:])
         ones = const.tile([P, P], BF16)
         nc.vector.memset(ones[:], 1.0)
-        rows = const.tile([P, DOUT + HEAD_COLS], BF16)
-        nc.vector.memset(rows[:].bitcast(I32), 0)
-        nc.scalar.dma_start(out=rows[0:1, 0:DOUT], in_=b_out.unsqueeze(0))
-        with nc.allow_non_contiguous_dma(reason="one element of each head's row"):
-            for row, table in ((W_ROW, w_mix), (B_ROW, b_mix)):
-                nc.scalar.dma_start(
-                    out=rows[0:1, DOUT + SLOT * row : DOUT + SLOT * row + HEADS],
-                    in_=table[:, index : index + 1].rearrange("h o -> o h"),
-                )
-        nc.scalar.dma_start(
-            out=rows[0:1, DOUT + SLOT * COEF_ROW : DOUT + SLOT * COEF_ROW + HEADS], in_=decay_values.unsqueeze(0)
-        )
-        proj_bias = const.tile([P, GROUPS, PACK], BF16)
-        nc.scalar.dma_start(
-            out=proj_bias[:], in_=b_proj.rearrange("h c -> (h c)").rearrange("(g q t) -> q g t", g=GROUPS, t=PACK)
-        )
-
-        out_bias = const.tile([P, DOUT], F32)
-        for n in range(OUT_TILES):
-            n_cols = slice(n * N_TILE, (n + 1) * N_TILE)
-            spread = psum.tile([P, N_TILE], F32, tag="bank")
-            nc.tensor.matmul(out=spread[:], lhsT=ones[:], rhs=rows[:, n_cols], start=True, stop=True)
-            nc.scalar.copy(out=out_bias[:, n_cols], in_=spread[:])
-        spread_heads = psum.tile([P, HEAD_COLS], F32, tag="bank")
-        nc.tensor.matmul(
-            out=spread_heads[:], lhsT=ones[:], rhs=rows[:, DOUT : DOUT + HEAD_COLS], start=True, stop=True
-        )
-        per_head = const.tile([P, 3, HEADS], F32)
-        nc.vector.tensor_copy(
-            out=per_head[:], in_=spread_heads[:].rearrange("p (r s) -> p r s", s=SLOT)[:, 0:3, 0:HEADS]
-        )
-        nc.vector.tensor_scalar(
-            out=per_head[:, COEF_ROW, :], in0=per_head[:, COEF_ROW, :],
-            scalar1=0.9, scalar2=1.0, op0=ALU.max, op1=ALU.min,
-        )
         exponent = const.tile([P, HEADS], F32)
         nc.vector.memset(exponent[:], decay_root)
-        nc.gpsimd.tensor_tensor(
-            out=per_head[:, COEF_ROW, :], in0=per_head[:, COEF_ROW, :], in1=exponent[:], op=ALU.pow
-        )
-        first_heads = slice(0, HEADS // 2)
-        nc.vector.tensor_tensor(
-            out=per_head[:, COEF_ROW, first_heads], in0=per_head[:, COEF_ROW, first_heads],
-            in1=per_head[:, W_ROW, first_heads], op=ALU.mult,
-        )
-        per_part = const.tile([P, 3, GROUPS], F32)
-        for hh in range(GROUP_HEADS):
-            parts = slice(hh * HEAD_PARTS, (hh + 1) * HEAD_PARTS)
-            nc.vector.tensor_copy(out=per_part[parts], in_=per_head[parts, :, hh:HEADS:GROUP_HEADS])
-        shift = const.tile([P, GROUPS, PACK], F32)
-        for g in range(GROUPS):
+        per_head = const.tile([P, 3, HEADS], F32)
+
+        def start_constants():
+            spread_heads = psum.tile([P, HEAD_COLS], F32, tag="bank")
+            nc.tensor.matmul(
+                out=spread_heads[:], lhsT=ones[:], rhs=rows[:, DOUT : DOUT + HEAD_COLS], start=True, stop=True
+            )
+            nc.vector.tensor_copy(
+                out=per_head[:], in_=spread_heads[:].rearrange("p (r s) -> p r s", s=SLOT)[:, 0:3, 0:HEADS]
+            )
             nc.vector.tensor_scalar(
-                out=shift[:, g, :], in0=proj_bias[:, g, :],
-                scalar1=per_part[:, W_ROW, g : g + 1], scalar2=per_part[:, B_ROW, g : g + 1],
-                op0=ALU.mult, op1=ALU.add,
+                out=per_head[:, COEF_ROW, :], in0=per_head[:, COEF_ROW, :],
+                scalar1=0.9, scalar2=1.0, op0=ALU.max, op1=ALU.min,
+            )
+            nc.gpsimd.tensor_tensor(
+                out=per_head[:, COEF_ROW, :], in0=per_head[:, COEF_ROW, :], in1=exponent[:], op=ALU.pow
             )
 
-        def quantise_weights(g):
-            w_codes = pair.tile([P, PASSES, PACK, P], U32, name="w_codes", align_bytes=64)
-            w_scales = pair.tile([P, PASSES, PACK, P], U8, name="w_scales", align_bytes=64)
-            for half in range(HALVES):
-                w_grouped = triple.tile([P, 2, PACK, P, PACK], BF16, name="w_grouped", align_bytes=64)
-                for hh in range(GROUP_HEADS):
-                    parts = slice(hh * HEAD_PARTS, (hh + 1) * HEAD_PARTS)
-                    for cc in range(2):
-                        sorted_view = w_grouped[:, cc, :, parts, :].rearrange("q t m j -> q m j t")
-                        raw_view = w_raw[(g, half)][:, hh, cc].rearrange("q j (m t) -> q m j t", t=PACK)
-                        if cc == 0:
-                            nc.vector.tensor_copy(out=sorted_view, in_=raw_view)
-                        else:
-                            nc.scalar.copy(out=sorted_view, in_=raw_view)
-                two = slice(2 * half, 2 * half + 2)
-                nc.vector.quantize_mx(
-                    out=w_codes[:, two].rearrange("q c t m -> q (c t m)").bitcast(FP8X4),
-                    scales=w_scales[:, two].rearrange("q c t m -> q (c t m)"),
-                    in_=w_grouped[:].rearrange("q c t m j -> q (c t m j)"),
-                )
-            return w_codes, w_scales
+        out_bias = const.tile([P, DOUT], F32)
 
-        first_weights = quantise_weights(0)
+        def spread_out_bias():
+            for n in range(OUT_TILES):
+                n_cols = slice(n * N_TILE, (n + 1) * N_TILE)
+                spread = psum.tile([P, N_TILE], F32, tag="bank")
+                nc.tensor.matmul(out=spread[:], lhsT=ones[:], rhs=rows[:, n_cols], start=True, stop=True)
+                nc.scalar.copy(out=out_bias[:, n_cols], in_=spread[:])
 
-        x_codes = keep.tile([P, BATCH_TILES, PASSES, P], U32, align_bytes=64)
-        x_scales = keep.tile([P, BATCH_TILES, PASSES, P], U8, align_bytes=64)
-        for i in range(BATCH_TILES):
-            x_words = x_sb[:, i, :].bitcast(F32)
-            x_grouped = pair.tile([P, PASSES, P, PACK], BF16, align_bytes=64)
-            for half in range(HALVES):
-                x_t = psum.tile([P, 2, 2, P], F32, tag="bank")
-                for cc in range(2):
-                    first = WORDS * (2 * half + cc)
-                    for u in range(2):
-                        nc.tensor.transpose(x_t[:, cc, u, :], x_words[:, first + u : first + WORDS : 2], ident[:])
-                nc.scalar.copy(
-                    out=x_grouped[:, 2 * half : 2 * half + 2].bitcast(F32), in_=x_t[:].rearrange("q c u p -> q c p u")
+        per_part = const.tile([P, 3, GROUPS], F32)
+        shift = const.tile([P, GROUPS, PACK], F32)
+
+        def finish_constants():
+            first_heads = slice(0, HEADS // 2)
+            nc.vector.tensor_tensor(
+                out=per_head[:, COEF_ROW, first_heads], in0=per_head[:, COEF_ROW, first_heads],
+                in1=per_head[:, W_ROW, first_heads], op=ALU.mult,
+            )
+            for hh in range(GROUP_HEADS):
+                parts = slice(hh * HEAD_PARTS, (hh + 1) * HEAD_PARTS)
+                nc.vector.tensor_copy(out=per_part[parts], in_=per_head[parts, :, hh:HEADS:GROUP_HEADS])
+            for g in range(GROUPS):
+                nc.vector.tensor_scalar(
+                    out=shift[:, g, :], in0=proj_bias[:, g, :],
+                    scalar1=per_part[:, W_ROW, g : g + 1], scalar2=per_part[:, B_ROW, g : g + 1],
+                    op0=ALU.mult, op1=ALU.add,
                 )
+
+        w_grouped = {}
+        w_codes = {}
+        w_scales = {}
+
+        def regroup(g, half, hh):
+            if hh == 0:
+                w_grouped[(g, half)] = triple.tile([P, 2, PACK, P, PACK], BF16, name="w_grouped", align_bytes=64)
+            parts = slice(hh * HEAD_PARTS, (hh + 1) * HEAD_PARTS)
+            for cc in range(2):
+                sorted_view = w_grouped[(g, half)][:, cc, :, parts, :].rearrange("q t m j -> q m j t")
+                raw_view = w_raw[(g, half)][:, hh, cc].rearrange("q j (m t) -> q m j t", t=PACK)
+                if cc == 0:
+                    nc.vector.tensor_copy(out=sorted_view, in_=raw_view)
+                else:
+                    nc.scalar.copy(out=sorted_view, in_=raw_view)
+
+        def quantise_weights(g, half):
+            if half == 0:
+                w_codes[g] = pair.tile([P, PASSES, PACK, P], U32, name="w_codes", align_bytes=64)
+                w_scales[g] = pair.tile([P, PASSES, PACK, P], U8, name="w_scales", align_bytes=64)
+            two = slice(2 * half, 2 * half + 2)
             nc.vector.quantize_mx(
-                out=x_codes[:, i].rearrange("q c p -> q (c p)").bitcast(FP8X4),
-                scales=x_scales[:, i].rearrange("q c p -> q (c p)"),
-                in_=x_grouped[:].rearrange("q c p t -> q (c p t)"),
+                out=w_codes[g][:, two].rearrange("q c t m -> q (c t m)").bitcast(FP8X4),
+                scales=w_scales[g][:, two].rearrange("q c t m -> q (c t m)"),
+                in_=w_grouped[(g, half)][:].rearrange("q c t m j -> q (c t m j)"),
             )
 
-        hid_codes = keep.tile([P, GROUPS, BATCH], U32, align_bytes=64)
-        hid_scales = keep.tile([P, GROUPS, BATCH], U8, align_bytes=64)
+        rest = {}
 
-        for g in range(GROUPS):
-            w_codes, w_scales = first_weights if g == 0 else quantise_weights(g)
-
-            rest = pair.tile([P, PACK, BATCH_TILES, P], F32)
+        def cache_term(g):
+            rest[g] = pair.tile([P, PACK, BATCH_TILES, P], F32, name="rest")
+            cache_t = [psum.tile([P, BATCH_TILES, P], F32, name="cache_t", tag="bank") for u in range(2)]
             for u in range(2):
-                cache_t = psum.tile([P, BATCH_TILES, P], F32, tag="bank")
                 for i in range(BATCH_TILES):
                     cache_words = cache_tiles[g][:, i].rearrange("p h n -> p (h n)").bitcast(F32)
-                    nc.tensor.transpose(cache_t[:, i, :], cache_words[:, u:WORDS:2], ident[:])
-                halves = cache_t[:].bitcast(BF16).rearrange("q i (p e) -> q i p e", e=2)
+                    nc.tensor.transpose(cache_t[u][:, i, :], cache_words[:, u:WORDS:2], ident[:])
+            for u in range(2):
+                halves = cache_t[u][:].bitcast(BF16).rearrange("q i (p e) -> q i p e", e=2)
                 for e in range(2):
                     t = 2 * u + e
                     nc.scalar.activation(
-                        out=rest[:, t], in_=halves[:, :, :, e], func=ACT.Identity,
+                        out=rest[g][:, t], in_=halves[:, :, :, e], func=ACT.Identity,
                         scale=per_part[:, COEF_ROW, g : g + 1], bias=shift[:, g, t : t + 1],
                     )
 
-            hid_grouped = pair.tile([P, BATCH_TILES, P, PACK], BF16, align_bytes=64)
+        def copy_out(turn, out_ap, in_ap):
+            if turn % 2 == 0:
+                nc.scalar.copy(out=out_ap, in_=in_ap)
+            else:
+                nc.vector.tensor_copy(out=out_ap, in_=in_ap)
+
+        x_codes = keep.tile([P, BATCH_TILES, PASSES, P], U32, align_bytes=64)
+        x_scales = keep.tile([P, BATCH_TILES, PASSES, P], U8, align_bytes=64)
+
+        def quantise_x():
             for i in range(BATCH_TILES):
-                proj = psum.tile([P, PACK, P], F32, tag="bank")
+                x_words = x_sb[:, i, :].bitcast(F32)
+                x_grouped = pair.tile([P, PASSES, P, PACK], BF16, name="x_grouped", align_bytes=64)
+                for half in range(HALVES):
+                    x_t = psum.tile([P, 2, 2, P], F32, name="x_t", tag="bank")
+                    for cc in range(2):
+                        first = WORDS * (2 * half + cc)
+                        for u in range(2):
+                            nc.tensor.transpose(x_t[:, cc, u, :], x_words[:, first + u : first + WORDS : 2], ident[:])
+                    copy_out(
+                        half, x_grouped[:, 2 * half : 2 * half + 2].bitcast(F32), x_t[:].rearrange("q c u p -> q c p u")
+                    )
+                nc.vector.quantize_mx(
+                    out=x_codes[:, i].rearrange("q c p -> q (c p)").bitcast(FP8X4),
+                    scales=x_scales[:, i].rearrange("q c p -> q (c p)"),
+                    in_=x_grouped[:].rearrange("q c p t -> q (c p t)"),
+                )
+
+        proj = {}
+
+        def first_product(g):
+            for i in range(BATCH_TILES):
+                proj[(g, i)] = psum.tile([P, PACK, P], F32, name="proj", tag="bank")
                 for t in range(PACK):
                     for c in range(PASSES):
                         nc.tensor.matmul_mx(
-                            out=proj[:, t, :],
-                            lhsT=w_codes[:, c, t, :].bitcast(FP8X4), lhsT_scale=w_scales[:, c, t, :],
+                            out=proj[(g, i)][:, t, :],
+                            lhsT=w_codes[g][:, c, t, :].bitcast(FP8X4), lhsT_scale=w_scales[g][:, c, t, :],
                             rhs=x_codes[:, i, c, :].bitcast(FP8X4), rhs_scale=x_scales[:, i, c, :],
                             start=(c == 0), stop=(c == PASSES - 1),
                         )
-                nc.vector.scalar_tensor_tensor(
-                    out=hid_grouped[:, i],
-                    in0=proj[:].rearrange("q t p -> q p t"), scalar=per_part[:, W_ROW, g : g + 1],
-                    in1=rest[:, :, i, :].rearrange("q t p -> q p t"),
-                    op0=ALU.mult, op1=ALU.add,
-                )
-            nc.vector.quantize_mx(
-                out=hid_codes[:, g, :].bitcast(FP8X4), scales=hid_scales[:, g, :],
-                in_=hid_grouped[:].rearrange("q i p t -> q (i p t)"),
+
+        hid_grouped = {}
+        hid_codes = keep.tile([P, GROUPS, BATCH], U32, align_bytes=64)
+        hid_scales = keep.tile([P, GROUPS, BATCH], U8, align_bytes=64)
+
+        def mix(g, i):
+            if i % 2 == 0:
+                hid_grouped[(g, i // 2)] = triple.tile([P, 2, P, PACK], BF16, name="hid_grouped", align_bytes=64)
+            nc.vector.scalar_tensor_tensor(
+                out=hid_grouped[(g, i // 2)][:, i % 2],
+                in0=proj[(g, i)][:].rearrange("q t p -> q p t"), scalar=per_part[:, W_ROW, g : g + 1],
+                in1=rest[g][:, :, i, :].rearrange("q t p -> q p t"),
+                op0=ALU.mult, op1=ALU.add,
             )
 
-        for n in range(OUT_TILES):
+        def quantise_hidden(g, i_pair):
+            cols = slice(2 * i_pair * P, 2 * (i_pair + 1) * P)
+            nc.vector.quantize_mx(
+                out=hid_codes[:, g, cols].bitcast(FP8X4), scales=hid_scales[:, g, cols],
+                in_=hid_grouped[(g, i_pair)][:].rearrange("q i p t -> q (i p t)"),
+            )
+
+        def prepare_and_mix(new, old):
+            if new is not None:
+                regroup(new, 0, 0)
+                regroup(new, 0, 1)
+                regroup(new, 1, 0)
+                quantise_weights(new, 0)
+                regroup(new, 1, 1)
+            mix(old, 0)
+            if new is not None:
+                quantise_weights(new, 1)
+            mix(old, 1)
+            mix(old, 2)
+            quantise_hidden(old, 0)
+            mix(old, 3)
+            quantise_hidden(old, 1)
+
+        regroup(0, 0, 0)
+        regroup(0, 0, 1)
+        start_constants()
+        regroup(0, 1, 0)
+        quantise_weights(0, 0)
+        regroup(0, 1, 1)
+        finish_constants()
+        quantise_weights(0, 1)
+        cache_term(0)
+        quantise_x()
+        for g in range(GROUPS):
+            if g > 0:
+                cache_term(g)
+            if g == GROUPS - 1:
+                spread_out_bias()
+            first_product(g)
+            prepare_and_mix(g + 1 if g + 1 < GROUPS else None, g)
+
+        def second_product_pass(acc, n, i, g):
+            nc.tensor.matmul_mx(
+                out=acc[:],
+                lhsT=hid_codes[:, g, i * P : (i + 1) * P].bitcast(FP8X4),
+                lhsT_scale=hid_scales[:, g, i * P : (i + 1) * P],
+                rhs=out_words[n][:, g, :].bitcast(FP8X4),
+                rhs_scale=out_scales[4 * g : P, n * N_TILE : (n + 1) * N_TILE],
+                start=(g == 0), stop=(g == GROUPS - 1),
+            )
+
+        def finish(acc, n, i):
             n_cols = slice(n * N_TILE, (n + 1) * N_TILE)
-            accs = [psum.tile([P, N_TILE], F32, name="acc", tag="bank") for i in range(BATCH_TILES)]
-            for g in range(GROUPS):
-                for i in range(BATCH_TILES):
-                    nc.tensor.matmul_mx(
-                        out=accs[i][:],
-                        lhsT=hid_codes[:, g, i * P : (i + 1) * P].bitcast(FP8X4),
-                        lhsT_scale=hid_scales[:, g, i * P : (i + 1) * P],
-                        rhs=out_words[n][:, g, :].bitcast(FP8X4),
-                        rhs_scale=out_scales[4 * g : P, n_cols],
-                        start=(g == 0), stop=(g == GROUPS - 1),
-                    )
+            result = store_pool.tile([P, N_TILE], F32, name="result")
+            nc.vector.tensor_tensor(out=result[:], in0=acc[:], in1=out_bias[:, n_cols], op=ALU.add)
+            nc.sync.dma_start(out=out_rows[:, i, n_cols], in_=result[:])
+
+        accs = [psum.tile([P, N_TILE], F32, name="acc", tag="bank") for i in range(BATCH_TILES)]
+        for g in range(GROUPS):
             for i in range(BATCH_TILES):
-                result = store_pool.tile([P, N_TILE], F32)
-                nc.vector.tensor_tensor(out=result[:], in0=accs[i][:], in1=out_bias[:, n_cols], op=ALU.add)
-                nc.sync.dma_start(out=out_rows[:, i, n_cols], in_=result[:])
+                second_product_pass(accs[i], 0, i, g)
+        for i in range(BATCH_TILES):
+            finish(accs[i], 0, i)
+        for n in range(1, OUT_TILES):
+            for i in range(BATCH_TILES):
+                acc = psum.tile([P, N_TILE], F32, tag="bank")
+                for g in range(GROUPS):
+                    second_product_pass(acc, n, i, g)
+                finish(acc, n, i)

@@ -41,7 +41,6 @@ def tile_mixedrepeatheads_kernel(
     out_rows = out.rearrange("(p i) n -> p i n", i=BATCH_TILES)
 
     with ExitStack() as ctx:
-        ctx.enter_context(tc.manual_schedule())
         const = ctx.enter_context(tc.tile_pool(name="const", bufs=1))
         keep = ctx.enter_context(tc.tile_pool(name="keep", bufs=1))
         ring = ctx.enter_context(tc.tile_pool(name="ring", bufs=GROUPS * HALVES))
@@ -66,37 +65,15 @@ def tile_mixedrepeatheads_kernel(
                 )
             return cache_sb
 
-        def load_small_vectors():
-            nc.sync.dma_start(out=rows[0:1, 0:DOUT], in_=b_out.unsqueeze(0))
-            with nc.allow_non_contiguous_dma(reason="one element of each head's row"):
-                for row, table in ((W_ROW, w_mix), (B_ROW, b_mix)):
-                    nc.sync.dma_start(
-                        out=rows[0:1, DOUT + SLOT * row : DOUT + SLOT * row + HEADS],
-                        in_=table[:, index : index + 1].rearrange("h o -> o h"),
-                    )
-            nc.sync.dma_start(
-                out=rows[0:1, DOUT + SLOT * COEF_ROW : DOUT + SLOT * COEF_ROW + HEADS], in_=decay_values.unsqueeze(0)
-            )
-            nc.sync.dma_start(
-                out=proj_bias[:], in_=b_proj.rearrange("h c -> (h c)").rearrange("(g q t) -> q g t", g=GROUPS, t=PACK)
-            )
-
-        rows = const.tile([P, DOUT + HEAD_COLS], BF16)
-        nc.vector.memset(rows[:].bitcast(I32), 0)
-        proj_bias = const.tile([P, GROUPS, PACK], BF16)
-
-        w_raw = {}
-        cache_tiles = []
+        w_raw = {(0, half): load_half_group(0, half) for half in range(HALVES)}
         x_sb = keep.tile([P, BATCH_TILES, DIM], BF16)
-        for g in range(GROUPS):
+        for i in range(BATCH_TILES):
+            nc.sync.dma_start(out=x_sb[:, i, :], in_=x_rows[:, i, :])
+        cache_tiles = [load_caches(0)]
+        for g in range(1, GROUPS):
             for half in range(HALVES):
                 w_raw[(g, half)] = load_half_group(g, half)
-                if (g, half) == (0, 0):
-                    load_small_vectors()
             cache_tiles.append(load_caches(g))
-            if g == 0:
-                for i in range(BATCH_TILES):
-                    nc.sync.dma_start(out=x_sb[:, i, :], in_=x_rows[:, i, :])
 
         out_scales = keep.tile([P, DOUT], U8, align_bytes=64)
         nc.vector.memset(out_scales[:].bitcast(I32), 0)
@@ -118,195 +95,148 @@ def tile_mixedrepeatheads_kernel(
         make_identity(nc, ident[:])
         ones = const.tile([P, P], BF16)
         nc.vector.memset(ones[:], 1.0)
-        exponent = const.tile([P, HEADS], F32)
-        nc.vector.memset(exponent[:], decay_root)
-        per_head = const.tile([P, 3, HEADS], F32)
-
-        def start_constants():
-            spread_heads = psum.tile([P, HEAD_COLS], F32, tag="bank")
-            nc.tensor.matmul(
-                out=spread_heads[:], lhsT=ones[:], rhs=rows[:, DOUT : DOUT + HEAD_COLS], start=True, stop=True
-            )
-            nc.vector.tensor_copy(
-                out=per_head[:], in_=spread_heads[:].rearrange("p (r s) -> p r s", s=SLOT)[:, 0:3, 0:HEADS]
-            )
-            nc.vector.tensor_scalar(
-                out=per_head[:, COEF_ROW, :], in0=per_head[:, COEF_ROW, :],
-                scalar1=0.9, scalar2=1.0, op0=ALU.max, op1=ALU.min,
-            )
-            nc.gpsimd.tensor_tensor(
-                out=per_head[:, COEF_ROW, :], in0=per_head[:, COEF_ROW, :], in1=exponent[:], op=ALU.pow
-            )
+        rows = const.tile([P, DOUT + HEAD_COLS], BF16)
+        nc.vector.memset(rows[:].bitcast(I32), 0)
+        nc.scalar.dma_start(out=rows[0:1, 0:DOUT], in_=b_out.unsqueeze(0))
+        with nc.allow_non_contiguous_dma(reason="one element of each head's row"):
+            for row, table in ((W_ROW, w_mix), (B_ROW, b_mix)):
+                nc.scalar.dma_start(
+                    out=rows[0:1, DOUT + SLOT * row : DOUT + SLOT * row + HEADS],
+                    in_=table[:, index : index + 1].rearrange("h o -> o h"),
+                )
+        nc.scalar.dma_start(
+            out=rows[0:1, DOUT + SLOT * COEF_ROW : DOUT + SLOT * COEF_ROW + HEADS], in_=decay_values.unsqueeze(0)
+        )
+        proj_bias = const.tile([P, GROUPS, PACK], BF16)
+        nc.scalar.dma_start(
+            out=proj_bias[:], in_=b_proj.rearrange("h c -> (h c)").rearrange("(g q t) -> q g t", g=GROUPS, t=PACK)
+        )
 
         out_bias = const.tile([P, DOUT], F32)
-
-        def spread_out_bias():
-            for n in range(OUT_TILES):
-                n_cols = slice(n * N_TILE, (n + 1) * N_TILE)
-                spread = psum.tile([P, N_TILE], F32, tag="bank")
-                nc.tensor.matmul(out=spread[:], lhsT=ones[:], rhs=rows[:, n_cols], start=True, stop=True)
-                nc.scalar.copy(out=out_bias[:, n_cols], in_=spread[:])
-
+        for n in range(OUT_TILES):
+            n_cols = slice(n * N_TILE, (n + 1) * N_TILE)
+            spread = psum.tile([P, N_TILE], F32, tag="bank")
+            nc.tensor.matmul(out=spread[:], lhsT=ones[:], rhs=rows[:, n_cols], start=True, stop=True)
+            nc.scalar.copy(out=out_bias[:, n_cols], in_=spread[:])
+        spread_heads = psum.tile([P, HEAD_COLS], F32, tag="bank")
+        nc.tensor.matmul(
+            out=spread_heads[:], lhsT=ones[:], rhs=rows[:, DOUT : DOUT + HEAD_COLS], start=True, stop=True
+        )
+        per_head = const.tile([P, 3, HEADS], F32)
+        nc.vector.tensor_copy(
+            out=per_head[:], in_=spread_heads[:].rearrange("p (r s) -> p r s", s=SLOT)[:, 0:3, 0:HEADS]
+        )
+        nc.vector.tensor_scalar(
+            out=per_head[:, COEF_ROW, :], in0=per_head[:, COEF_ROW, :],
+            scalar1=0.9, scalar2=1.0, op0=ALU.max, op1=ALU.min,
+        )
+        exponent = const.tile([P, HEADS], F32)
+        nc.vector.memset(exponent[:], decay_root)
+        nc.gpsimd.tensor_tensor(
+            out=per_head[:, COEF_ROW, :], in0=per_head[:, COEF_ROW, :], in1=exponent[:], op=ALU.pow
+        )
+        first_heads = slice(0, HEADS // 2)
+        nc.vector.tensor_tensor(
+            out=per_head[:, COEF_ROW, first_heads], in0=per_head[:, COEF_ROW, first_heads],
+            in1=per_head[:, W_ROW, first_heads], op=ALU.mult,
+        )
         per_part = const.tile([P, 3, GROUPS], F32)
-        shift = const.tile([P, GROUPS, PACK], F32)
-
-        def finish_constants():
-            first_heads = slice(0, HEADS // 2)
-            nc.vector.tensor_tensor(
-                out=per_head[:, COEF_ROW, first_heads], in0=per_head[:, COEF_ROW, first_heads],
-                in1=per_head[:, W_ROW, first_heads], op=ALU.mult,
-            )
-            for hh in range(GROUP_HEADS):
-                parts = slice(hh * HEAD_PARTS, (hh + 1) * HEAD_PARTS)
-                nc.vector.tensor_copy(out=per_part[parts], in_=per_head[parts, :, hh:HEADS:GROUP_HEADS])
-            for g in range(GROUPS):
-                nc.vector.tensor_scalar(
-                    out=shift[:, g, :], in0=proj_bias[:, g, :],
-                    scalar1=per_part[:, W_ROW, g : g + 1], scalar2=per_part[:, B_ROW, g : g + 1],
-                    op0=ALU.mult, op1=ALU.add,
-                )
-
-        w_grouped = {}
-        w_codes = {}
-        w_scales = {}
-
-        def regroup(g, half, hh):
-            if hh == 0:
-                w_grouped[(g, half)] = triple.tile([P, 2, PACK, P, PACK], BF16, name="w_grouped", align_bytes=64)
+        for hh in range(GROUP_HEADS):
             parts = slice(hh * HEAD_PARTS, (hh + 1) * HEAD_PARTS)
-            for cc in range(2):
-                sorted_view = w_grouped[(g, half)][:, cc, :, parts, :].rearrange("q t m j -> q m j t")
-                raw_view = w_raw[(g, half)][:, hh, cc].rearrange("q j (m t) -> q m j t", t=PACK)
-                if cc == 0:
-                    nc.vector.tensor_copy(out=sorted_view, in_=raw_view)
-                else:
-                    nc.scalar.copy(out=sorted_view, in_=raw_view)
-
-        def quantise_weights(g, half):
-            if half == 0:
-                w_codes[g] = pair.tile([P, PASSES, PACK, P], U32, name="w_codes", align_bytes=64)
-                w_scales[g] = pair.tile([P, PASSES, PACK, P], U8, name="w_scales", align_bytes=64)
-            two = slice(2 * half, 2 * half + 2)
-            nc.vector.quantize_mx(
-                out=w_codes[g][:, two].rearrange("q c t m -> q (c t m)").bitcast(FP8X4),
-                scales=w_scales[g][:, two].rearrange("q c t m -> q (c t m)"),
-                in_=w_grouped[(g, half)][:].rearrange("q c t m j -> q (c t m j)"),
-            )
-
-        rest = {}
-
-        def cache_term(g):
-            rest[g] = pair.tile([P, PACK, BATCH_TILES, P], F32, name="rest")
-            cache_t = [psum.tile([P, BATCH_TILES, P], F32, name="cache_t", tag="bank") for u in range(2)]
-            for u in range(2):
-                for i in range(BATCH_TILES):
-                    cache_words = cache_tiles[g][:, i].rearrange("p h n -> p (h n)").bitcast(F32)
-                    nc.tensor.transpose(cache_t[u][:, i, :], cache_words[:, u:WORDS:2], ident[:])
-            for u in range(2):
-                halves = cache_t[u][:].bitcast(BF16).rearrange("q i (p e) -> q i p e", e=2)
-                for e in range(2):
-                    t = 2 * u + e
-                    nc.scalar.activation(
-                        out=rest[g][:, t], in_=halves[:, :, :, e], func=ACT.Identity,
-                        scale=per_part[:, COEF_ROW, g : g + 1], bias=shift[:, g, t : t + 1],
-                    )
-
-        def copy_out(turn, out_ap, in_ap):
-            if turn % 2 == 0:
-                nc.scalar.copy(out=out_ap, in_=in_ap)
-            else:
-                nc.vector.tensor_copy(out=out_ap, in_=in_ap)
-
-        x_codes = keep.tile([P, BATCH_TILES, PASSES, P], U32, align_bytes=64)
-        x_scales = keep.tile([P, BATCH_TILES, PASSES, P], U8, align_bytes=64)
-
-        def quantise_x():
-            for i in range(BATCH_TILES):
-                x_words = x_sb[:, i, :].bitcast(F32)
-                x_grouped = pair.tile([P, PASSES, P, PACK], BF16, name="x_grouped", align_bytes=64)
-                for half in range(HALVES):
-                    x_t = psum.tile([P, 2, 2, P], F32, name="x_t", tag="bank")
-                    for cc in range(2):
-                        first = WORDS * (2 * half + cc)
-                        for u in range(2):
-                            nc.tensor.transpose(x_t[:, cc, u, :], x_words[:, first + u : first + WORDS : 2], ident[:])
-                    copy_out(
-                        half, x_grouped[:, 2 * half : 2 * half + 2].bitcast(F32), x_t[:].rearrange("q c u p -> q c p u")
-                    )
-                nc.vector.quantize_mx(
-                    out=x_codes[:, i].rearrange("q c p -> q (c p)").bitcast(FP8X4),
-                    scales=x_scales[:, i].rearrange("q c p -> q (c p)"),
-                    in_=x_grouped[:].rearrange("q c p t -> q (c p t)"),
-                )
-
-        proj = {}
-
-        def first_product(g):
-            for i in range(BATCH_TILES):
-                proj[(g, i)] = psum.tile([P, PACK, P], F32, name="proj", tag="bank")
-                for t in range(PACK):
-                    for c in range(PASSES):
-                        nc.tensor.matmul_mx(
-                            out=proj[(g, i)][:, t, :],
-                            lhsT=w_codes[g][:, c, t, :].bitcast(FP8X4), lhsT_scale=w_scales[g][:, c, t, :],
-                            rhs=x_codes[:, i, c, :].bitcast(FP8X4), rhs_scale=x_scales[:, i, c, :],
-                            start=(c == 0), stop=(c == PASSES - 1),
-                        )
-
-        hid_grouped = {}
-        hid_codes = keep.tile([P, GROUPS, BATCH], U32, align_bytes=64)
-        hid_scales = keep.tile([P, GROUPS, BATCH], U8, align_bytes=64)
-
-        def mix(g, i):
-            if i % 2 == 0:
-                hid_grouped[(g, i // 2)] = triple.tile([P, 2, P, PACK], BF16, name="hid_grouped", align_bytes=64)
-            nc.vector.scalar_tensor_tensor(
-                out=hid_grouped[(g, i // 2)][:, i % 2],
-                in0=proj[(g, i)][:].rearrange("q t p -> q p t"), scalar=per_part[:, W_ROW, g : g + 1],
-                in1=rest[g][:, :, i, :].rearrange("q t p -> q p t"),
+            nc.vector.tensor_copy(out=per_part[parts], in_=per_head[parts, :, hh:HEADS:GROUP_HEADS])
+        shift = const.tile([P, GROUPS, PACK], F32)
+        for g in range(GROUPS):
+            nc.vector.tensor_scalar(
+                out=shift[:, g, :], in0=proj_bias[:, g, :],
+                scalar1=per_part[:, W_ROW, g : g + 1], scalar2=per_part[:, B_ROW, g : g + 1],
                 op0=ALU.mult, op1=ALU.add,
             )
 
-        def quantise_hidden(g, i_pair):
-            cols = slice(2 * i_pair * P, 2 * (i_pair + 1) * P)
+        def quantise_weights(g):
+            w_codes = pair.tile([P, PASSES, PACK, P], U32, name="w_codes", align_bytes=64)
+            w_scales = pair.tile([P, PASSES, PACK, P], U8, name="w_scales", align_bytes=64)
+            for half in range(HALVES):
+                w_grouped = triple.tile([P, 2, PACK, P, PACK], BF16, name="w_grouped", align_bytes=64)
+                for hh in range(GROUP_HEADS):
+                    parts = slice(hh * HEAD_PARTS, (hh + 1) * HEAD_PARTS)
+                    for cc in range(2):
+                        sorted_view = w_grouped[:, cc, :, parts, :].rearrange("q t m j -> q m j t")
+                        raw_view = w_raw[(g, half)][:, hh, cc].rearrange("q j (m t) -> q m j t", t=PACK)
+                        if cc == 0:
+                            nc.vector.tensor_copy(out=sorted_view, in_=raw_view)
+                        else:
+                            nc.scalar.copy(out=sorted_view, in_=raw_view)
+                two = slice(2 * half, 2 * half + 2)
+                nc.vector.quantize_mx(
+                    out=w_codes[:, two].rearrange("q c t m -> q (c t m)").bitcast(FP8X4),
+                    scales=w_scales[:, two].rearrange("q c t m -> q (c t m)"),
+                    in_=w_grouped[:].rearrange("q c t m j -> q (c t m j)"),
+                )
+            return w_codes, w_scales
+
+        first_weights = quantise_weights(0)
+
+        x_codes = keep.tile([P, BATCH_TILES, PASSES, P], U32, align_bytes=64)
+        x_scales = keep.tile([P, BATCH_TILES, PASSES, P], U8, align_bytes=64)
+        for i in range(BATCH_TILES):
+            x_words = x_sb[:, i, :].bitcast(F32)
+            x_grouped = pair.tile([P, PASSES, P, PACK], BF16, align_bytes=64)
+            for half in range(HALVES):
+                x_t = psum.tile([P, 2, 2, P], F32, tag="bank")
+                for cc in range(2):
+                    first = WORDS * (2 * half + cc)
+                    for u in range(2):
+                        nc.tensor.transpose(x_t[:, cc, u, :], x_words[:, first + u : first + WORDS : 2], ident[:])
+                nc.scalar.copy(
+                    out=x_grouped[:, 2 * half : 2 * half + 2].bitcast(F32), in_=x_t[:].rearrange("q c u p -> q c p u")
+                )
             nc.vector.quantize_mx(
-                out=hid_codes[:, g, cols].bitcast(FP8X4), scales=hid_scales[:, g, cols],
-                in_=hid_grouped[(g, i_pair)][:].rearrange("q i p t -> q (i p t)"),
+                out=x_codes[:, i].rearrange("q c p -> q (c p)").bitcast(FP8X4),
+                scales=x_scales[:, i].rearrange("q c p -> q (c p)"),
+                in_=x_grouped[:].rearrange("q c p t -> q (c p t)"),
             )
 
-        def prepare_and_mix(new, old):
-            if new is not None:
-                regroup(new, 0, 0)
-                regroup(new, 0, 1)
-                regroup(new, 1, 0)
-                quantise_weights(new, 0)
-                regroup(new, 1, 1)
-            mix(old, 0)
-            if new is not None:
-                quantise_weights(new, 1)
-            mix(old, 1)
-            mix(old, 2)
-            quantise_hidden(old, 0)
-            mix(old, 3)
-            quantise_hidden(old, 1)
+        hid_codes = keep.tile([P, GROUPS, BATCH], U32, align_bytes=64)
+        hid_scales = keep.tile([P, GROUPS, BATCH], U8, align_bytes=64)
 
-        regroup(0, 0, 0)
-        regroup(0, 0, 1)
-        start_constants()
-        regroup(0, 1, 0)
-        quantise_weights(0, 0)
-        regroup(0, 1, 1)
-        finish_constants()
-        quantise_weights(0, 1)
-        cache_term(0)
-        quantise_x()
         for g in range(GROUPS):
-            if g > 0:
-                cache_term(g)
-            if g == GROUPS - 1:
-                spread_out_bias()
-            first_product(g)
-            prepare_and_mix(g + 1 if g + 1 < GROUPS else None, g)
+            w_codes, w_scales = first_weights if g == 0 else quantise_weights(g)
+
+            rest = pair.tile([P, PACK, BATCH_TILES, P], F32)
+            for u in range(2):
+                cache_t = psum.tile([P, BATCH_TILES, P], F32, tag="bank")
+                for i in range(BATCH_TILES):
+                    cache_words = cache_tiles[g][:, i].rearrange("p h n -> p (h n)").bitcast(F32)
+                    nc.tensor.transpose(cache_t[:, i, :], cache_words[:, u:WORDS:2], ident[:])
+                halves = cache_t[:].bitcast(BF16).rearrange("q i (p e) -> q i p e", e=2)
+                for e in range(2):
+                    t = 2 * u + e
+                    nc.scalar.activation(
+                        out=rest[:, t], in_=halves[:, :, :, e], func=ACT.Identity,
+                        scale=per_part[:, COEF_ROW, g : g + 1], bias=shift[:, g, t : t + 1],
+                    )
+
+            hid_grouped = pair.tile([P, BATCH_TILES, P, PACK], BF16, align_bytes=64)
+            for i in range(BATCH_TILES):
+                proj = psum.tile([P, PACK, P], F32, tag="bank")
+                for t in range(PACK):
+                    for c in range(PASSES):
+                        nc.tensor.matmul_mx(
+                            out=proj[:, t, :],
+                            lhsT=w_codes[:, c, t, :].bitcast(FP8X4), lhsT_scale=w_scales[:, c, t, :],
+                            rhs=x_codes[:, i, c, :].bitcast(FP8X4), rhs_scale=x_scales[:, i, c, :],
+                            start=(c == 0), stop=(c == PASSES - 1),
+                        )
+                nc.vector.scalar_tensor_tensor(
+                    out=hid_grouped[:, i],
+                    in0=proj[:].rearrange("q t p -> q p t"), scalar=per_part[:, W_ROW, g : g + 1],
+                    in1=rest[:, :, i, :].rearrange("q t p -> q p t"),
+                    op0=ALU.mult, op1=ALU.add,
+                )
+            nc.vector.quantize_mx(
+                out=hid_codes[:, g, :].bitcast(FP8X4), scales=hid_scales[:, g, :],
+                in_=hid_grouped[:].rearrange("q i p t -> q (i p t)"),
+            )
 
         def second_product_pass(acc, n, i, g):
             nc.tensor.matmul_mx(

@@ -41,6 +41,7 @@ def tile_mixedrepeatheads_kernel(
     out_rows = out.rearrange("(p i) n -> p i n", i=BATCH_TILES)
 
     with ExitStack() as ctx:
+        ctx.enter_context(tc.manual_schedule())
         const = ctx.enter_context(tc.tile_pool(name="const", bufs=1))
         keep = ctx.enter_context(tc.tile_pool(name="keep", bufs=1))
         ring = ctx.enter_context(tc.tile_pool(name="ring", bufs=GROUPS * HALVES))
@@ -48,6 +49,22 @@ def tile_mixedrepeatheads_kernel(
         triple = ctx.enter_context(tc.tile_pool(name="triple", bufs=3))
         store_pool = ctx.enter_context(tc.tile_pool(name="store", bufs=8))
         psum = ctx.enter_context(tc.psum_pool(name="psum", bufs=8))
+
+        head_rows = const.tile([P, HEAD_COLS], BF16)
+        nc.vector.memset(head_rows[:].bitcast(I32), 0)
+        exponent = const.tile([P, HEADS], F32)
+        nc.vector.memset(exponent[:], decay_root)
+        ones = const.tile([P, P], BF16)
+        nc.vector.memset(ones[:], 1.0)
+        table_probe = const.tile([P, 1], F32)
+        nc.scalar.activation(out=table_probe[:], in_=exponent[:, 0:1], func=ACT.Identity)
+        ident = const.tile([P, P], F32)
+        make_identity(nc, ident[:])
+        bias_row = const.tile([P, DOUT], BF16)
+        nc.gpsimd.memset(bias_row[:].bitcast(I32), 0)
+        nc.gpsimd.dma_start(out=bias_row[0:1, :], in_=b_out.unsqueeze(0))
+        out_scales = keep.tile([P, DOUT], U8, align_bytes=64)
+        nc.gpsimd.memset(out_scales[:].bitcast(I32), 0)
 
         def load_half_group(g, half):
             raw = ring.tile([P, GROUP_HEADS, 2, PACK, HID], BF16, name="raw", tag="weights", align_bytes=64)
@@ -66,17 +83,37 @@ def tile_mixedrepeatheads_kernel(
             return cache_sb
 
         w_raw = {(0, half): load_half_group(0, half) for half in range(HALVES)}
+        with nc.allow_non_contiguous_dma(reason="one element of each head's row"):
+            for row, table in ((W_ROW, w_mix), (B_ROW, b_mix)):
+                nc.sync.dma_start(
+                    out=head_rows[0:1, SLOT * row : SLOT * row + HEADS],
+                    in_=table[:, index : index + 1].rearrange("h o -> o h"),
+                )
+        nc.sync.dma_start(
+            out=head_rows[0:1, SLOT * COEF_ROW : SLOT * COEF_ROW + HEADS], in_=decay_values.unsqueeze(0)
+        )
+        proj_bias = const.tile([P, GROUPS, PACK], BF16)
+        nc.sync.dma_start(
+            out=proj_bias[:], in_=b_proj.rearrange("h c -> (h c)").rearrange("(g q t) -> q g t", g=GROUPS, t=PACK)
+        )
         x_sb = keep.tile([P, BATCH_TILES, DIM], BF16)
-        for i in range(BATCH_TILES):
+        cache_tiles = {}
+
+        def load_x(i):
             nc.sync.dma_start(out=x_sb[:, i, :], in_=x_rows[:, i, :])
-        cache_tiles = [load_caches(0)]
-        for g in range(1, GROUPS):
+
+        load_x(0)
+        load_x(1)
+        w_raw[(1, 0)] = load_half_group(1, 0)
+        load_x(2)
+        load_x(3)
+        w_raw[(1, 1)] = load_half_group(1, 1)
+        cache_tiles[0] = load_caches(0)
+        cache_tiles[1] = load_caches(1)
+        for g in range(2, GROUPS):
             for half in range(HALVES):
                 w_raw[(g, half)] = load_half_group(g, half)
-            cache_tiles.append(load_caches(g))
-
-        out_scales = keep.tile([P, DOUT], U8, align_bytes=64)
-        nc.vector.memset(out_scales[:].bitcast(I32), 0)
+            cache_tiles[g] = load_caches(g)
         for quadrant in range(4):
             nc.sync.dma_start(
                 out=out_scales[32 * quadrant : 32 * quadrant + 4 * GROUPS, :].bitcast(I32),
@@ -91,151 +128,147 @@ def tile_mixedrepeatheads_kernel(
             )
             out_words.append(words)
 
-        ident = const.tile([P, P], F32)
-        make_identity(nc, ident[:])
-        ones = const.tile([P, P], BF16)
-        nc.vector.memset(ones[:], 1.0)
-        rows = const.tile([P, DOUT + HEAD_COLS], BF16)
-        nc.vector.memset(rows[:].bitcast(I32), 0)
-        nc.scalar.dma_start(out=rows[0:1, 0:DOUT], in_=b_out.unsqueeze(0))
-        with nc.allow_non_contiguous_dma(reason="one element of each head's row"):
-            for row, table in ((W_ROW, w_mix), (B_ROW, b_mix)):
-                nc.scalar.dma_start(
-                    out=rows[0:1, DOUT + SLOT * row : DOUT + SLOT * row + HEADS],
-                    in_=table[:, index : index + 1].rearrange("h o -> o h"),
+        per_head = const.tile([P, 3, HEADS], F32)
+        per_part = const.tile([P, 3, GROUPS], F32)
+        shift = const.tile([P, GROUPS, PACK], F32)
+
+        def spread_heads():
+            spread = psum.tile([P, HEAD_COLS], F32, name="spread", tag="bank")
+            nc.tensor.matmul(out=spread[:], lhsT=ones[:], rhs=head_rows[:], start=True, stop=True)
+            nc.scalar.copy(out=per_head[:], in_=spread[:].rearrange("p (r s) -> p r s", s=SLOT)[:, 0:3, 0:HEADS])
+            nc.gpsimd.tensor_scalar(
+                out=per_head[:, COEF_ROW, :], in0=per_head[:, COEF_ROW, :],
+                scalar1=0.9, scalar2=1.0, op0=ALU.max, op1=ALU.min,
+            )
+            nc.gpsimd.tensor_tensor(
+                out=per_head[:, COEF_ROW, :], in0=per_head[:, COEF_ROW, :], in1=exponent[:], op=ALU.pow
+            )
+            first_heads = slice(0, HEADS // 2)
+            nc.gpsimd.tensor_tensor(
+                out=per_head[:, COEF_ROW, first_heads], in0=per_head[:, COEF_ROW, first_heads],
+                in1=per_head[:, W_ROW, first_heads], op=ALU.mult,
+            )
+            for hh in range(GROUP_HEADS):
+                parts = slice(hh * HEAD_PARTS, (hh + 1) * HEAD_PARTS)
+                nc.gpsimd.tensor_copy(out=per_part[parts], in_=per_head[parts, :, hh:HEADS:GROUP_HEADS])
+            for g in range(GROUPS):
+                nc.gpsimd.tensor_scalar(
+                    out=shift[:, g, :], in0=proj_bias[:, g, :],
+                    scalar1=per_part[:, W_ROW, g : g + 1], scalar2=per_part[:, B_ROW, g : g + 1],
+                    op0=ALU.mult, op1=ALU.add,
                 )
-        nc.scalar.dma_start(
-            out=rows[0:1, DOUT + SLOT * COEF_ROW : DOUT + SLOT * COEF_ROW + HEADS], in_=decay_values.unsqueeze(0)
-        )
-        proj_bias = const.tile([P, GROUPS, PACK], BF16)
-        nc.scalar.dma_start(
-            out=proj_bias[:], in_=b_proj.rearrange("h c -> (h c)").rearrange("(g q t) -> q g t", g=GROUPS, t=PACK)
-        )
 
         out_bias = const.tile([P, DOUT], F32)
-        for n in range(OUT_TILES):
+
+        def spread_out_bias(n, copy):
             n_cols = slice(n * N_TILE, (n + 1) * N_TILE)
-            spread = psum.tile([P, N_TILE], F32, tag="bank")
-            nc.tensor.matmul(out=spread[:], lhsT=ones[:], rhs=rows[:, n_cols], start=True, stop=True)
-            nc.scalar.copy(out=out_bias[:, n_cols], in_=spread[:])
-        spread_heads = psum.tile([P, HEAD_COLS], F32, tag="bank")
-        nc.tensor.matmul(
-            out=spread_heads[:], lhsT=ones[:], rhs=rows[:, DOUT : DOUT + HEAD_COLS], start=True, stop=True
-        )
-        per_head = const.tile([P, 3, HEADS], F32)
-        nc.vector.tensor_copy(
-            out=per_head[:], in_=spread_heads[:].rearrange("p (r s) -> p r s", s=SLOT)[:, 0:3, 0:HEADS]
-        )
-        nc.vector.tensor_scalar(
-            out=per_head[:, COEF_ROW, :], in0=per_head[:, COEF_ROW, :],
-            scalar1=0.9, scalar2=1.0, op0=ALU.max, op1=ALU.min,
-        )
-        exponent = const.tile([P, HEADS], F32)
-        nc.vector.memset(exponent[:], decay_root)
-        nc.gpsimd.tensor_tensor(
-            out=per_head[:, COEF_ROW, :], in0=per_head[:, COEF_ROW, :], in1=exponent[:], op=ALU.pow
-        )
-        first_heads = slice(0, HEADS // 2)
-        nc.vector.tensor_tensor(
-            out=per_head[:, COEF_ROW, first_heads], in0=per_head[:, COEF_ROW, first_heads],
-            in1=per_head[:, W_ROW, first_heads], op=ALU.mult,
-        )
-        per_part = const.tile([P, 3, GROUPS], F32)
-        for hh in range(GROUP_HEADS):
-            parts = slice(hh * HEAD_PARTS, (hh + 1) * HEAD_PARTS)
-            nc.vector.tensor_copy(out=per_part[parts], in_=per_head[parts, :, hh:HEADS:GROUP_HEADS])
-        shift = const.tile([P, GROUPS, PACK], F32)
-        for g in range(GROUPS):
-            nc.vector.tensor_scalar(
-                out=shift[:, g, :], in0=proj_bias[:, g, :],
-                scalar1=per_part[:, W_ROW, g : g + 1], scalar2=per_part[:, B_ROW, g : g + 1],
-                op0=ALU.mult, op1=ALU.add,
-            )
+            spread = psum.tile([P, N_TILE], F32, name="spread", tag="bank")
+            nc.tensor.matmul(out=spread[:], lhsT=ones[:], rhs=bias_row[:, n_cols], start=True, stop=True)
+            copy(out=out_bias[:, n_cols], in_=spread[:])
 
-        def quantise_weights(g):
-            w_codes = pair.tile([P, PASSES, PACK, P], U32, name="w_codes", align_bytes=64)
-            w_scales = pair.tile([P, PASSES, PACK, P], U8, name="w_scales", align_bytes=64)
-            for half in range(HALVES):
-                w_grouped = triple.tile([P, 2, PACK, P, PACK], BF16, name="w_grouped", align_bytes=64)
-                for hh in range(GROUP_HEADS):
-                    parts = slice(hh * HEAD_PARTS, (hh + 1) * HEAD_PARTS)
-                    for cc in range(2):
-                        sorted_view = w_grouped[:, cc, :, parts, :].rearrange("q t m j -> q m j t")
-                        raw_view = w_raw[(g, half)][:, hh, cc].rearrange("q j (m t) -> q m j t", t=PACK)
-                        if cc == 0:
-                            nc.vector.tensor_copy(out=sorted_view, in_=raw_view)
-                        else:
-                            nc.scalar.copy(out=sorted_view, in_=raw_view)
-                two = slice(2 * half, 2 * half + 2)
-                nc.vector.quantize_mx(
-                    out=w_codes[:, two].rearrange("q c t m -> q (c t m)").bitcast(FP8X4),
-                    scales=w_scales[:, two].rearrange("q c t m -> q (c t m)"),
-                    in_=w_grouped[:].rearrange("q c t m j -> q (c t m j)"),
+        w_grouped, w_codes, w_scales = {}, {}, {}
+
+        def regroup(g, half, hh):
+            if hh == 0:
+                w_grouped[(g, half)] = triple.tile(
+                    [P, 2, PACK, P, PACK], BF16, name="w_grouped", tag="w_grouped", align_bytes=64
                 )
-            return w_codes, w_scales
+            parts = slice(hh * HEAD_PARTS, (hh + 1) * HEAD_PARTS)
+            for cc, copy in ((0, nc.vector.tensor_copy), (1, nc.scalar.copy)):
+                copy(
+                    out=w_grouped[(g, half)][:, cc, :, parts, :].rearrange("q t m j -> q m j t"),
+                    in_=w_raw[(g, half)][:, hh, cc].rearrange("q j (m t) -> q m j t", t=PACK),
+                )
 
-        first_weights = quantise_weights(0)
+        def quantise_weights(g, half):
+            if half == 0:
+                w_codes[g] = pair.tile([P, PASSES, PACK, P], U32, name="w_codes", tag="w_codes", align_bytes=64)
+                w_scales[g] = pair.tile([P, PASSES, PACK, P], U8, name="w_scales", tag="w_scales", align_bytes=64)
+            two = slice(2 * half, 2 * half + 2)
+            nc.vector.quantize_mx(
+                out=w_codes[g][:, two].rearrange("q c t m -> q (c t m)").bitcast(FP8X4),
+                scales=w_scales[g][:, two].rearrange("q c t m -> q (c t m)"),
+                in_=w_grouped[(g, half)][:].rearrange("q c t m j -> q (c t m j)"),
+            )
 
         x_codes = keep.tile([P, BATCH_TILES, PASSES, P], U32, align_bytes=64)
         x_scales = keep.tile([P, BATCH_TILES, PASSES, P], U8, align_bytes=64)
-        for i in range(BATCH_TILES):
+        x_grouped = {}
+
+        def turn_x(i):
             x_words = x_sb[:, i, :].bitcast(F32)
-            x_grouped = pair.tile([P, PASSES, P, PACK], BF16, align_bytes=64)
+            x_grouped[i] = triple.tile([P, PASSES, P, PACK], BF16, name="x_grouped", tag="x_grouped", align_bytes=64)
             for half in range(HALVES):
-                x_t = psum.tile([P, 2, 2, P], F32, tag="bank")
+                x_t = psum.tile([P, 2, 2, P], F32, name="x_t", tag="bank")
                 for cc in range(2):
                     first = WORDS * (2 * half + cc)
                     for u in range(2):
                         nc.tensor.transpose(x_t[:, cc, u, :], x_words[:, first + u : first + WORDS : 2], ident[:])
-                nc.scalar.copy(
-                    out=x_grouped[:, 2 * half : 2 * half + 2].bitcast(F32), in_=x_t[:].rearrange("q c u p -> q c p u")
+                copy = nc.vector.tensor_copy if half == 1 and i > 0 else nc.scalar.copy
+                copy(
+                    out=x_grouped[i][:, 2 * half : 2 * half + 2].bitcast(F32),
+                    in_=x_t[:].rearrange("q c u p -> q c p u"),
                 )
+
+        def quantise_x(i):
             nc.vector.quantize_mx(
                 out=x_codes[:, i].rearrange("q c p -> q (c p)").bitcast(FP8X4),
                 scales=x_scales[:, i].rearrange("q c p -> q (c p)"),
-                in_=x_grouped[:].rearrange("q c p t -> q (c p t)"),
+                in_=x_grouped[i][:].rearrange("q c p t -> q (c p t)"),
             )
 
+        rest, hid_grouped, proj = {}, {}, {}
         hid_codes = keep.tile([P, GROUPS, BATCH], U32, align_bytes=64)
         hid_scales = keep.tile([P, GROUPS, BATCH], U8, align_bytes=64)
 
-        for g in range(GROUPS):
-            w_codes, w_scales = first_weights if g == 0 else quantise_weights(g)
+        cache_t = {}
 
-            rest = pair.tile([P, PACK, BATCH_TILES, P], F32)
+        def turn_caches(g, step):
+            if step == 1:
+                rest[g] = triple.tile([P, PACK, BATCH_TILES, P], F32, name="rest", tag="rest")
             for u in range(2):
-                cache_t = psum.tile([P, BATCH_TILES, P], F32, tag="bank")
-                for i in range(BATCH_TILES):
-                    cache_words = cache_tiles[g][:, i].rearrange("p h n -> p (h n)").bitcast(F32)
-                    nc.tensor.transpose(cache_t[:, i, :], cache_words[:, u:WORDS:2], ident[:])
-                halves = cache_t[:].bitcast(BF16).rearrange("q i (p e) -> q i p e", e=2)
-                for e in range(2):
-                    t = 2 * u + e
-                    nc.scalar.activation(
-                        out=rest[:, t], in_=halves[:, :, :, e], func=ACT.Identity,
-                        scale=per_part[:, COEF_ROW, g : g + 1], bias=shift[:, g, t : t + 1],
+                if step == 0:
+                    cache_t[(g, u)] = psum.tile([P, BATCH_TILES, P], F32, name="cache_t", tag="bank")
+                    for i in range(BATCH_TILES):
+                        cache_words = cache_tiles[g][:, i].rearrange("p h n -> p (h n)").bitcast(F32)
+                        nc.tensor.transpose(cache_t[(g, u)][:, i, :], cache_words[:, u:WORDS:2], ident[:])
+                else:
+                    halves = cache_t[(g, u)][:].bitcast(BF16).rearrange("q i (p e) -> q i p e", e=2)
+                    for e in range(2):
+                        t = 2 * u + e
+                        nc.scalar.activation(
+                            out=rest[g][:, t], in_=halves[:, :, :, e], func=ACT.Identity,
+                            scale=per_part[:, COEF_ROW, g : g + 1], bias=shift[:, g, t : t + 1],
+                        )
+
+        def project(g, i):
+            proj[(g, i)] = psum.tile([P, PACK, P], F32, name="proj", tag="bank")
+            for t in range(PACK):
+                for c in range(PASSES):
+                    nc.tensor.matmul_mx(
+                        out=proj[(g, i)][:, t, :],
+                        lhsT=w_codes[g][:, c, t, :].bitcast(FP8X4), lhsT_scale=w_scales[g][:, c, t, :],
+                        rhs=x_codes[:, i, c, :].bitcast(FP8X4), rhs_scale=x_scales[:, i, c, :],
+                        start=(c == 0), stop=(c == PASSES - 1),
                     )
 
-            hid_grouped = pair.tile([P, BATCH_TILES, P, PACK], BF16, align_bytes=64)
-            for i in range(BATCH_TILES):
-                proj = psum.tile([P, PACK, P], F32, tag="bank")
-                for t in range(PACK):
-                    for c in range(PASSES):
-                        nc.tensor.matmul_mx(
-                            out=proj[:, t, :],
-                            lhsT=w_codes[:, c, t, :].bitcast(FP8X4), lhsT_scale=w_scales[:, c, t, :],
-                            rhs=x_codes[:, i, c, :].bitcast(FP8X4), rhs_scale=x_scales[:, i, c, :],
-                            start=(c == 0), stop=(c == PASSES - 1),
-                        )
-                nc.vector.scalar_tensor_tensor(
-                    out=hid_grouped[:, i],
-                    in0=proj[:].rearrange("q t p -> q p t"), scalar=per_part[:, W_ROW, g : g + 1],
-                    in1=rest[:, :, i, :].rearrange("q t p -> q p t"),
-                    op0=ALU.mult, op1=ALU.add,
+        def mix(g, i):
+            if i == 0:
+                hid_grouped[g] = pair.tile(
+                    [P, BATCH_TILES, P, PACK], BF16, name="hid_grouped", tag="hid_grouped", align_bytes=64
                 )
+            nc.vector.scalar_tensor_tensor(
+                out=hid_grouped[g][:, i],
+                in0=proj[(g, i)][:].rearrange("q t p -> q p t"), scalar=per_part[:, W_ROW, g : g + 1],
+                in1=rest[g][:, :, i, :].rearrange("q t p -> q p t"),
+                op0=ALU.mult, op1=ALU.add,
+            )
+
+        def quantise_hidden(g, tiles):
+            cols = slice(tiles.start * P, tiles.stop * P)
             nc.vector.quantize_mx(
-                out=hid_codes[:, g, :].bitcast(FP8X4), scales=hid_scales[:, g, :],
-                in_=hid_grouped[:].rearrange("q i p t -> q (i p t)"),
+                out=hid_codes[:, g, cols].bitcast(FP8X4), scales=hid_scales[:, g, cols],
+                in_=hid_grouped[g][:, tiles].rearrange("q i p t -> q (i p t)"),
             )
 
         def second_product_pass(acc, n, i, g):
@@ -254,15 +287,94 @@ def tile_mixedrepeatheads_kernel(
             nc.vector.tensor_tensor(out=result[:], in0=acc[:], in1=out_bias[:, n_cols], op=ALU.add)
             nc.sync.dma_start(out=out_rows[:, i, n_cols], in_=result[:])
 
-        accs = [psum.tile([P, N_TILE], F32, name="acc", tag="bank") for i in range(BATCH_TILES)]
-        for g in range(GROUPS):
-            for i in range(BATCH_TILES):
-                second_product_pass(accs[i], 0, i, g)
+        regroup(0, 0, 0)
+        regroup(0, 0, 1)
+        quantise_weights(0, 0)
+        regroup(0, 1, 0)
+        spread_heads()
+        regroup(0, 1, 1)
+        turn_x(0)
+        quantise_weights(0, 1)
+        turn_x(1)
+        quantise_x(0)
+        regroup(1, 0, 0)
+        quantise_x(1)
+        regroup(1, 0, 1)
+        turn_x(2)
+        quantise_weights(1, 0)
+        turn_x(3)
+        quantise_x(2)
+        regroup(1, 1, 0)
+        quantise_x(3)
+        regroup(1, 1, 1)
+        quantise_weights(1, 1)
+        project(0, 0)
+        project(0, 1)
+        turn_caches(0, 0)
+        project(0, 2)
+        project(0, 3)
+        turn_caches(1, 0)
+        turn_caches(0, 1)
         for i in range(BATCH_TILES):
-            finish(accs[i], 0, i)
+            mix(0, i)
+        for i in range(BATCH_TILES):
+            project(1, i)
+        turn_caches(2, 0)
+        regroup(2, 0, 0)
+        regroup(2, 0, 1)
+        quantise_hidden(0, slice(0, BATCH_TILES))
+        regroup(2, 1, 0)
+        quantise_weights(2, 0)
+        regroup(2, 1, 1)
+        quantise_weights(2, 1)
+        turn_caches(1, 1)
+        turn_caches(2, 1)
+        for i in range(BATCH_TILES):
+            mix(1, i)
+        for i in range(BATCH_TILES):
+            project(2, i)
+        turn_caches(3, 0)
+        regroup(3, 0, 0)
+        regroup(3, 0, 1)
+        quantise_hidden(1, slice(0, BATCH_TILES))
+        mix(2, 0)
+        mix(2, 1)
+        quantise_weights(3, 0)
+        mix(2, 2)
+        mix(2, 3)
+        regroup(3, 1, 0)
+        quantise_hidden(2, slice(0, BATCH_TILES))
+        regroup(3, 1, 1)
+        quantise_weights(3, 1)
+        turn_caches(3, 1)
+        for n in range(2):
+            spread_out_bias(n, nc.scalar.copy)
+
+        accs = {}
+        early = [(0, i) for i in range(BATCH_TILES)] + [(1, 0), (1, 1)]
+        for n, i in early:
+            accs[(n, i)] = psum.tile([P, N_TILE], F32, name="acc", tag="bank")
+            for g in range(GROUPS - 2):
+                second_product_pass(accs[(n, i)], n, i, g)
+        for n, i in early:
+            second_product_pass(accs[(n, i)], n, i, GROUPS - 2)
+        for i in range(BATCH_TILES):
+            project(GROUPS - 1, i)
+            mix(GROUPS - 1, i)
+            if i >= 1:
+                quantise_hidden(GROUPS - 1, slice(i - 1, i))
+        quantise_hidden(GROUPS - 1, slice(3, 4))
+        for i in range(BATCH_TILES):
+            for n in range(2):
+                if (n, i) in early:
+                    second_product_pass(accs[(n, i)], n, i, GROUPS - 1)
+                    finish(accs[(n, i)], n, i)
+        for n in range(2, OUT_TILES):
+            spread_out_bias(n, nc.scalar.copy)
         for n in range(1, OUT_TILES):
             for i in range(BATCH_TILES):
-                acc = psum.tile([P, N_TILE], F32, tag="bank")
-                for g in range(GROUPS):
-                    second_product_pass(acc, n, i, g)
-                finish(acc, n, i)
+                if (n, i) not in early:
+                    acc = psum.tile([P, N_TILE], F32, name="acc", tag="bank")
+                    for g in range(GROUPS):
+                        second_product_pass(acc, n, i, g)
+                    finish(acc, n, i)

@@ -60,9 +60,6 @@ def tile_mixedrepeatheads_kernel(
         nc.scalar.activation(out=table_probe[:], in_=exponent[:, 0:1], func=ACT.Identity)
         ident = const.tile([P, P], F32)
         make_identity(nc, ident[:])
-        bias_row = const.tile([P, DOUT], BF16)
-        nc.gpsimd.memset(bias_row[:].bitcast(I32), 0)
-        nc.gpsimd.dma_start(out=bias_row[0:1, :], in_=b_out.unsqueeze(0))
         out_scales = keep.tile([P, DOUT], U8, align_bytes=64)
         nc.gpsimd.memset(out_scales[:].bitcast(I32), 0)
 
@@ -121,7 +118,10 @@ def tile_mixedrepeatheads_kernel(
             )
         word_bytes = W_out_words.rearrange("g q n t -> q g (n t)")
         out_words = []
+        out_bias = const.tile([P, DOUT], BF16)
         for n in range(OUT_TILES):
+            if n == OUT_TILES // 2:
+                nc.sync.dma_start(out=out_bias[:], in_=b_out.partition_broadcast(P))
             words = ring.tile([P, GROUPS, N_TILE], U32, name="words", tag="weights", align_bytes=64)
             nc.sync.dma_start(
                 out=words[:].bitcast(I32), in_=word_bytes[:, :, PACK * n * N_TILE : PACK * (n + 1) * N_TILE].bitcast(I32)
@@ -157,14 +157,6 @@ def tile_mixedrepeatheads_kernel(
                     scalar1=per_part[:, W_ROW, g : g + 1], scalar2=per_part[:, B_ROW, g : g + 1],
                     op0=ALU.mult, op1=ALU.add,
                 )
-
-        out_bias = const.tile([P, DOUT], F32)
-
-        def spread_out_bias(n, copy):
-            n_cols = slice(n * N_TILE, (n + 1) * N_TILE)
-            spread = psum.tile([P, N_TILE], F32, name="spread", tag="bank")
-            nc.tensor.matmul(out=spread[:], lhsT=ones[:], rhs=bias_row[:, n_cols], start=True, stop=True)
-            copy(out=out_bias[:, n_cols], in_=spread[:])
 
         w_grouped, w_codes, w_scales = {}, {}, {}
 
@@ -347,8 +339,6 @@ def tile_mixedrepeatheads_kernel(
         regroup(3, 1, 1)
         quantise_weights(3, 1)
         turn_caches(3, 1)
-        for n in range(2):
-            spread_out_bias(n, nc.scalar.copy)
 
         accs = {}
         early = [(0, i) for i in range(BATCH_TILES)] + [(1, 0), (1, 1)]
@@ -369,8 +359,6 @@ def tile_mixedrepeatheads_kernel(
                 if (n, i) in early:
                     second_product_pass(accs[(n, i)], n, i, GROUPS - 1)
                     finish(accs[(n, i)], n, i)
-        for n in range(2, OUT_TILES):
-            spread_out_bias(n, nc.scalar.copy)
         for n in range(1, OUT_TILES):
             for i in range(BATCH_TILES):
                 if (n, i) not in early:

@@ -24,6 +24,9 @@ GROUP_HEADS = HEADS // GROUPS
 HEAD_PARTS = HID // PACK
 N_TILE = 512
 OUT_TILES = DOUT // N_TILE
+SIDES = 2
+SIDE_COLS = DOUT // SIDES
+N_PER_SIDE = SIDE_COLS // N_TILE
 WORDS = K_PASS // 2
 SLOT = 16
 HEAD_COLS = 64
@@ -116,17 +119,21 @@ def tile_mixedrepeatheads_kernel(
                 out=out_scales[32 * quadrant : 32 * quadrant + 4 * GROUPS, :].bitcast(I32),
                 in_=W_out_scales[:, 4 * quadrant : 4 * quadrant + 4, :].bitcast(I32),
             )
-        word_bytes = W_out_words.rearrange("g q n t -> q g (n t)")
-        out_words = []
+        out_words = {}
         out_bias = const.tile([P, DOUT], BF16)
-        for n in range(OUT_TILES):
-            if n == OUT_TILES // 2:
+        for side in range(SIDES):
+            side_cols = slice(side * SIDE_COLS, (side + 1) * SIDE_COLS)
+            for g in range(GROUPS):
+                if g % 2 == 0:
+                    words = ring.tile([P, 2, SIDE_COLS], U32, name="words", tag="weights", align_bytes=64)
+                nc.sync.dma_start(
+                    out=words[:, g % 2, :].bitcast(I32),
+                    in_=W_out_words[g, :, side_cols, :].rearrange("q n t -> q (n t)").bitcast(I32),
+                )
+                for half in range(N_PER_SIDE):
+                    out_words[(side * N_PER_SIDE + half, g)] = words[:, g % 2, half * N_TILE : (half + 1) * N_TILE]
+            if side == 0:
                 nc.sync.dma_start(out=out_bias[:], in_=b_out.partition_broadcast(P))
-            words = ring.tile([P, GROUPS, N_TILE], U32, name="words", tag="weights", align_bytes=64)
-            nc.sync.dma_start(
-                out=words[:].bitcast(I32), in_=word_bytes[:, :, PACK * n * N_TILE : PACK * (n + 1) * N_TILE].bitcast(I32)
-            )
-            out_words.append(words)
 
         per_head = const.tile([P, 3, HEADS], F32)
         per_part = const.tile([P, 3, GROUPS], F32)
@@ -186,6 +193,11 @@ def tile_mixedrepeatheads_kernel(
         x_codes = keep.tile([P, BATCH_TILES, PASSES, P], U32, align_bytes=64)
         x_scales = keep.tile([P, BATCH_TILES, PASSES, P], U8, align_bytes=64)
         x_grouped = {}
+
+        def keep_busy(passes, columns):
+            idle = psum.tile([P, N_TILE], F32, name="idle", tag="bank")
+            for step in range(passes):
+                nc.tensor.matmul(out=idle[:], lhsT=ones[:], rhs=columns, start=True, stop=True)
 
         def turn_x(i):
             x_words = x_sb[:, i, :].bitcast(F32)
@@ -268,7 +280,7 @@ def tile_mixedrepeatheads_kernel(
                 out=acc[:],
                 lhsT=hid_codes[:, g, i * P : (i + 1) * P].bitcast(FP8X4),
                 lhsT_scale=hid_scales[:, g, i * P : (i + 1) * P],
-                rhs=out_words[n][:, g, :].bitcast(FP8X4),
+                rhs=out_words[(n, g)].bitcast(FP8X4),
                 rhs_scale=out_scales[4 * g : P, n * N_TILE : (n + 1) * N_TILE],
                 start=(g == 0), stop=(g == GROUPS - 1),
             )
@@ -285,14 +297,18 @@ def tile_mixedrepeatheads_kernel(
         regroup(0, 1, 0)
         spread_heads()
         regroup(0, 1, 1)
+        keep_busy(4, w_raw[(0, 1)][:, 0].rearrange("q c j n -> q (c j n)")[:, 0:N_TILE])
         turn_x(0)
+        keep_busy(2, x_sb[:, 0, 0:N_TILE])
         quantise_weights(0, 1)
         turn_x(1)
+        keep_busy(4, x_sb[:, 1, 0:N_TILE])
         quantise_x(0)
         regroup(1, 0, 0)
         quantise_x(1)
         regroup(1, 0, 1)
         turn_x(2)
+        keep_busy(2, x_sb[:, 2, 0:N_TILE])
         quantise_weights(1, 0)
         turn_x(3)
         quantise_x(2)
@@ -342,12 +358,11 @@ def tile_mixedrepeatheads_kernel(
 
         accs = {}
         early = [(0, i) for i in range(BATCH_TILES)] + [(1, 0), (1, 1)]
-        for n, i in early:
-            accs[(n, i)] = psum.tile([P, N_TILE], F32, name="acc", tag="bank")
-            for g in range(GROUPS - 2):
+        for g in range(GROUPS - 1):
+            for n, i in early:
+                if g == 0:
+                    accs[(n, i)] = psum.tile([P, N_TILE], F32, name="acc", tag="bank")
                 second_product_pass(accs[(n, i)], n, i, g)
-        for n, i in early:
-            second_product_pass(accs[(n, i)], n, i, GROUPS - 2)
         for i in range(BATCH_TILES):
             project(GROUPS - 1, i)
             mix(GROUPS - 1, i)

@@ -167,13 +167,13 @@ def tile_mixedrepeatheads_kernel(
 
         w_grouped, w_codes, w_scales = {}, {}, {}
 
-        def regroup(g, half, hh):
+        def regroup(g, half, hh, all_scalar=False):
             if hh == 0:
                 w_grouped[(g, half)] = triple.tile(
                     [P, 2, PACK, P, PACK], BF16, name="w_grouped", tag="w_grouped", align_bytes=64
                 )
             parts = slice(hh * HEAD_PARTS, (hh + 1) * HEAD_PARTS)
-            for cc, copy in ((0, nc.vector.tensor_copy), (1, nc.scalar.copy)):
+            for cc, copy in ((0, nc.scalar.copy if all_scalar else nc.vector.tensor_copy), (1, nc.scalar.copy)):
                 copy(
                     out=w_grouped[(g, half)][:, cc, :, parts, :].rearrange("q t m j -> q m j t"),
                     in_=w_raw[(g, half)][:, hh, cc].rearrange("q j (m t) -> q m j t", t=PACK),
@@ -208,7 +208,7 @@ def tile_mixedrepeatheads_kernel(
                     first = WORDS * (2 * half + cc)
                     for u in range(2):
                         nc.tensor.transpose(x_t[:, cc, u, :], x_words[:, first + u : first + WORDS : 2], ident[:])
-                copy = nc.vector.tensor_copy if half == 1 and i > 0 else nc.scalar.copy
+                copy = nc.vector.tensor_copy if half == 1 and i > 1 else nc.scalar.copy
                 copy(
                     out=x_grouped[i][:, 2 * half : 2 * half + 2].bitcast(F32),
                     in_=x_t[:].rearrange("q c u p -> q c p u"),
@@ -275,21 +275,22 @@ def tile_mixedrepeatheads_kernel(
                 in_=hid_grouped[g][:, tiles].rearrange("q i p t -> q (i p t)"),
             )
 
-        def second_product_pass(acc, n, i, g):
+        def second_product_pass(acc, n, i, g, cols=slice(0, N_TILE)):
+            out_cols = slice(n * N_TILE + cols.start, n * N_TILE + cols.stop)
             nc.tensor.matmul_mx(
-                out=acc[:],
+                out=acc[:, cols],
                 lhsT=hid_codes[:, g, i * P : (i + 1) * P].bitcast(FP8X4),
                 lhsT_scale=hid_scales[:, g, i * P : (i + 1) * P],
-                rhs=out_words[(n, g)].bitcast(FP8X4),
-                rhs_scale=out_scales[4 * g : P, n * N_TILE : (n + 1) * N_TILE],
+                rhs=out_words[(n, g)][:, cols].bitcast(FP8X4),
+                rhs_scale=out_scales[4 * g : P, out_cols],
                 start=(g == 0), stop=(g == GROUPS - 1),
             )
 
-        def finish(acc, n, i):
-            n_cols = slice(n * N_TILE, (n + 1) * N_TILE)
+        def finish(acc, n, i, cols=slice(0, N_TILE)):
+            out_cols = slice(n * N_TILE + cols.start, n * N_TILE + cols.stop)
             result = store_pool.tile([P, N_TILE], F32, name="result")
-            nc.vector.tensor_tensor(out=result[:], in0=acc[:], in1=out_bias[:, n_cols], op=ALU.add)
-            nc.sync.dma_start(out=out_rows[:, i, n_cols], in_=result[:])
+            nc.vector.tensor_tensor(out=result[:, cols], in0=acc[:, cols], in1=out_bias[:, out_cols], op=ALU.add)
+            nc.sync.dma_start(out=out_rows[:, i, out_cols], in_=result[:, cols])
 
         regroup(0, 0, 0)
         regroup(0, 0, 1)
@@ -330,29 +331,27 @@ def tile_mixedrepeatheads_kernel(
         turn_caches(2, 0)
         regroup(2, 0, 0)
         regroup(2, 0, 1)
-        quantise_hidden(0, slice(0, BATCH_TILES))
-        regroup(2, 1, 0)
         quantise_weights(2, 0)
-        regroup(2, 1, 1)
+        regroup(2, 1, 0)
+        regroup(2, 1, 1, all_scalar=True)
         quantise_weights(2, 1)
+        quantise_hidden(0, slice(0, BATCH_TILES))
         turn_caches(1, 1)
-        turn_caches(2, 1)
+        regroup(3, 0, 0)
+        regroup(3, 0, 1)
         for i in range(BATCH_TILES):
             mix(1, i)
+        turn_caches(2, 1)
         for i in range(BATCH_TILES):
             project(2, i)
         turn_caches(3, 0)
-        regroup(3, 0, 0)
-        regroup(3, 0, 1)
-        quantise_hidden(1, slice(0, BATCH_TILES))
-        mix(2, 0)
-        mix(2, 1)
         quantise_weights(3, 0)
-        mix(2, 2)
-        mix(2, 3)
+        quantise_hidden(1, slice(0, BATCH_TILES))
+        for i in range(BATCH_TILES):
+            mix(2, i)
         regroup(3, 1, 0)
+        regroup(3, 1, 1, all_scalar=True)
         quantise_hidden(2, slice(0, BATCH_TILES))
-        regroup(3, 1, 1)
         quantise_weights(3, 1)
         turn_caches(3, 1)
 
@@ -377,7 +376,10 @@ def tile_mixedrepeatheads_kernel(
         for n in range(1, OUT_TILES):
             for i in range(BATCH_TILES):
                 if (n, i) not in early:
-                    acc = psum.tile([P, N_TILE], F32, name="acc", tag="bank")
-                    for g in range(GROUPS):
-                        second_product_pass(acc, n, i, g)
-                    finish(acc, n, i)
+                    width = N_TILE // 2 if (n, i) == (OUT_TILES - 1, BATCH_TILES - 1) else N_TILE
+                    for first in range(0, N_TILE, width):
+                        cols = slice(first, first + width)
+                        acc = psum.tile([P, N_TILE], F32, name="acc", tag="bank")
+                        for g in range(GROUPS):
+                            second_product_pass(acc, n, i, g, cols)
+                        finish(acc, n, i, cols)

@@ -110,10 +110,11 @@ def tile_mixedrepeatheads_kernel(
         w_raw[(1, 1)] = load_half_group(1, 1)
         cache_tiles[0] = load_caches(0)
         cache_tiles[1] = load_caches(1)
-        for g in range(2, GROUPS):
-            for half in range(HALVES):
-                w_raw[(g, half)] = load_half_group(g, half)
-            cache_tiles[g] = load_caches(g)
+        for half in range(HALVES):
+            w_raw[(2, half)] = load_half_group(2, half)
+        cache_tiles[2] = load_caches(2)
+        for half in range(HALVES):
+            w_raw[(3, half)] = load_half_group(3, half)
         for quadrant in range(4):
             nc.sync.dma_start(
                 out=out_scales[32 * quadrant : 32 * quadrant + 4 * GROUPS, :].bitcast(I32),
@@ -130,8 +131,10 @@ def tile_mixedrepeatheads_kernel(
                     out=words[:, g % 2, :].bitcast(I32),
                     in_=W_out_words[g, :, side_cols, :].rearrange("q n t -> q (n t)").bitcast(I32),
                 )
-                for half in range(N_PER_SIDE):
-                    out_words[(side * N_PER_SIDE + half, g)] = words[:, g % 2, half * N_TILE : (half + 1) * N_TILE]
+                for part in range(N_PER_SIDE):
+                    out_words[(side * N_PER_SIDE + part, g)] = words[:, g % 2, part * N_TILE : (part + 1) * N_TILE]
+                if (side, g) == (0, 1):
+                    cache_tiles[3] = load_caches(3)
             if side == 0:
                 nc.sync.dma_start(out=out_bias[:], in_=b_out.partition_broadcast(P))
 
@@ -314,8 +317,8 @@ def tile_mixedrepeatheads_kernel(
         turn_x(3)
         quantise_x(2)
         regroup(1, 1, 0)
-        quantise_x(3)
         regroup(1, 1, 1)
+        quantise_x(3)
         quantise_weights(1, 1)
         project(0, 0)
         project(0, 1)
@@ -331,11 +334,11 @@ def tile_mixedrepeatheads_kernel(
         turn_caches(2, 0)
         regroup(2, 0, 0)
         regroup(2, 0, 1)
-        quantise_weights(2, 0)
         regroup(2, 1, 0)
+        quantise_weights(2, 0)
         regroup(2, 1, 1, all_scalar=True)
-        quantise_weights(2, 1)
         quantise_hidden(0, slice(0, BATCH_TILES))
+        quantise_weights(2, 1)
         turn_caches(1, 1)
         regroup(3, 0, 0)
         regroup(3, 0, 1)
@@ -344,7 +347,6 @@ def tile_mixedrepeatheads_kernel(
         turn_caches(2, 1)
         for i in range(BATCH_TILES):
             project(2, i)
-        turn_caches(3, 0)
         quantise_weights(3, 0)
         quantise_hidden(1, slice(0, BATCH_TILES))
         for i in range(BATCH_TILES):
@@ -353,11 +355,13 @@ def tile_mixedrepeatheads_kernel(
         regroup(3, 1, 1, all_scalar=True)
         quantise_hidden(2, slice(0, BATCH_TILES))
         quantise_weights(3, 1)
-        turn_caches(3, 1)
 
         accs = {}
         early = [(0, i) for i in range(BATCH_TILES)] + [(1, 0), (1, 1)]
         for g in range(GROUPS - 1):
+            if g == GROUPS - 2:
+                turn_caches(GROUPS - 1, 0)
+                turn_caches(GROUPS - 1, 1)
             for n, i in early:
                 if g == 0:
                     accs[(n, i)] = psum.tile([P, N_TILE], F32, name="acc", tag="bank")

@@ -135,8 +135,7 @@ def tile_mixedrepeatheads_kernel(
                     out_words[(side * N_PER_SIDE + part, g)] = words[:, g % 2, part * N_TILE : (part + 1) * N_TILE]
                 if (side, g) == (0, 1):
                     cache_tiles[3] = load_caches(3)
-            if side == 0:
-                nc.sync.dma_start(out=out_bias[:], in_=b_out.partition_broadcast(P))
+        nc.sync.dma_start(out=out_bias[:], in_=b_out.partition_broadcast(P))
 
         per_head = const.tile([P, 3, HEADS], F32)
         per_part = const.tile([P, 3, GROUPS], F32)

@@ -339,20 +339,21 @@ def tile_mixedrepeatheads_kernel(
         quantise_hidden(0, slice(0, BATCH_TILES))
         quantise_weights(2, 1)
         turn_caches(1, 1)
+        turn_caches(2, 1)
         regroup(3, 0, 0)
         regroup(3, 0, 1)
         for i in range(BATCH_TILES):
             mix(1, i)
-        turn_caches(2, 1)
         for i in range(BATCH_TILES):
             project(2, i)
-        quantise_weights(3, 0)
+        mix(2, 0)
         quantise_hidden(1, slice(0, BATCH_TILES))
-        for i in range(BATCH_TILES):
+        for i in range(1, BATCH_TILES):
             mix(2, i)
+        quantise_weights(3, 0)
+        quantise_hidden(2, slice(0, BATCH_TILES))
         regroup(3, 1, 0)
         regroup(3, 1, 1, all_scalar=True)
-        quantise_hidden(2, slice(0, BATCH_TILES))
         quantise_weights(3, 1)
 
         accs = {}

@@ -196,11 +196,6 @@ def tile_mixedrepeatheads_kernel(
         x_scales = keep.tile([P, BATCH_TILES, PASSES, P], U8, align_bytes=64)
         x_grouped = {}
 
-        def keep_busy(passes, columns):
-            idle = psum.tile([P, N_TILE], F32, name="idle", tag="bank")
-            for step in range(passes):
-                nc.tensor.matmul(out=idle[:], lhsT=ones[:], rhs=columns, start=True, stop=True)
-
         def turn_x(i):
             x_words = x_sb[:, i, :].bitcast(F32)
             x_grouped[i] = triple.tile([P, PASSES, P, PACK], BF16, name="x_grouped", tag="x_grouped", align_bytes=64)
@@ -300,27 +295,23 @@ def tile_mixedrepeatheads_kernel(
         regroup(0, 1, 0)
         spread_heads()
         regroup(0, 1, 1)
-        keep_busy(4, w_raw[(0, 1)][:, 0].rearrange("q c j n -> q (c j n)")[:, 0:N_TILE])
         turn_x(0)
-        keep_busy(2, x_sb[:, 0, 0:N_TILE])
         quantise_weights(0, 1)
         turn_x(1)
-        keep_busy(4, x_sb[:, 1, 0:N_TILE])
         quantise_x(0)
         regroup(1, 0, 0)
         quantise_x(1)
         regroup(1, 0, 1)
         turn_x(2)
-        keep_busy(2, x_sb[:, 2, 0:N_TILE])
         quantise_weights(1, 0)
+        project(0, 0)
         turn_x(3)
+        project(0, 1)
         quantise_x(2)
         regroup(1, 1, 0)
         regroup(1, 1, 1)
         quantise_x(3)
         quantise_weights(1, 1)
-        project(0, 0)
-        project(0, 1)
         turn_caches(0, 0)
         project(0, 2)
         project(0, 3)

@@ -17,8 +17,10 @@ PACK = 4
 K_PASS = P * PACK
 BATCH, DIM, HID, HEADS, DOUT = 512, 2048, 256, 8, 2048
 BATCH_TILES = BATCH // P
+PAIR = 2 * P
+PAIRS = BATCH // PAIR
 PASSES = DIM // K_PASS
-HALVES = PASSES // 2
+HALVES = 2
 GROUPS = HEADS * HID // K_PASS
 GROUP_HEADS = HEADS // GROUPS
 HEAD_PARTS = HID // PACK
@@ -50,8 +52,12 @@ def tile_mixedrepeatheads_kernel(
         ring = ctx.enter_context(tc.tile_pool(name="ring", bufs=GROUPS * HALVES))
         pair = ctx.enter_context(tc.tile_pool(name="pair", bufs=2))
         triple = ctx.enter_context(tc.tile_pool(name="triple", bufs=3))
+        quad = ctx.enter_context(tc.tile_pool(name="quad", bufs=GROUPS))
         store_pool = ctx.enter_context(tc.tile_pool(name="store", bufs=8))
-        psum = ctx.enter_context(tc.psum_pool(name="psum", bufs=8))
+        psum = ctx.enter_context(tc.psum_pool(name="psum", bufs=1))
+
+        def bank(number, shape, dtype, name):
+            return psum.tile(shape, dtype, name=name, tag="bank%d" % number)
 
         head_rows = const.tile([P, HEAD_COLS], BF16)
         nc.vector.memset(head_rows[:].bitcast(I32), 0)
@@ -63,86 +69,107 @@ def tile_mixedrepeatheads_kernel(
         nc.scalar.activation(out=table_probe[:], in_=exponent[:, 0:1], func=ACT.Identity)
         ident = const.tile([P, P], F32)
         make_identity(nc, ident[:])
+        ident_bf = const.tile([P, P], BF16)
+        make_identity(nc, ident_bf[:])
         out_scales = keep.tile([P, DOUT], U8, align_bytes=64)
         nc.gpsimd.memset(out_scales[:].bitcast(I32), 0)
 
-        def load_half_group(g, half):
+        w_raw, cache_tiles, out_words = {}, {}, {}
+        proj_bias = const.tile([P, GROUPS, PACK], BF16)
+        x_sb = keep.tile([P, BATCH_TILES, DIM], BF16)
+        out_bias = const.tile([P, DOUT], BF16)
+
+        def load_half_group(g, half, split=1):
             raw = ring.tile([P, GROUP_HEADS, 2, PACK, HID], BF16, name="raw", tag="weights", align_bytes=64)
             for hh in range(GROUP_HEADS):
                 by_pass = W_proj[GROUP_HEADS * g + hh].rearrange("(c q j) n -> q c j n", c=PASSES, j=PACK)
-                nc.sync.dma_start(out=raw[:, hh], in_=by_pass[:, 2 * half : 2 * half + 2])
-            return raw
+                for part in range(split):
+                    passes = slice(part * 2 // split, (part + 1) * 2 // split)
+                    nc.sync.dma_start(
+                        out=raw[:, hh, passes],
+                        in_=by_pass[:, 2 * half + passes.start : 2 * half + passes.stop],
+                    )
+            w_raw[(g, half)] = raw
+
+        def load_x(half):
+            cols = slice(half * DIM // HALVES, (half + 1) * DIM // HALVES)
+            for r in range(PAIRS):
+                tiles = slice(2 * r, 2 * r + 2)
+                nc.sync.dma_start(out=x_sb[:, tiles, cols], in_=x_rows[:, tiles, cols])
+
+        def load_vectors():
+            with nc.allow_non_contiguous_dma(reason="one element of each head's row"):
+                for row, table in ((W_ROW, w_mix), (B_ROW, b_mix)):
+                    nc.sync.dma_start(
+                        out=head_rows[0:1, SLOT * row : SLOT * row + HEADS],
+                        in_=table[:, index : index + 1].rearrange("h o -> o h"),
+                    )
+            nc.sync.dma_start(
+                out=head_rows[0:1, SLOT * COEF_ROW : SLOT * COEF_ROW + HEADS], in_=decay_values.unsqueeze(0)
+            )
+            nc.sync.dma_start(
+                out=proj_bias[:],
+                in_=b_proj.rearrange("h c -> (h c)").rearrange("(g q t) -> q g t", g=GROUPS, t=PACK),
+            )
 
         def load_caches(g):
-            cache_sb = keep.tile([P, BATCH_TILES, GROUP_HEADS, HID], BF16, name="cache_sb%d" % g)
+            cache_tiles[g] = keep.tile([P, BATCH_TILES, GROUP_HEADS, HID], BF16, name="cache_sb%d" % g)
             for hh in range(GROUP_HEADS):
                 nc.sync.dma_start(
-                    out=cache_sb[:, :, hh, :],
+                    out=cache_tiles[g][:, :, hh, :],
                     in_=caches[GROUP_HEADS * g + hh].rearrange("(p i) n -> p i n", i=BATCH_TILES),
                 )
-            return cache_sb
 
-        w_raw = {(0, half): load_half_group(0, half) for half in range(HALVES)}
-        with nc.allow_non_contiguous_dma(reason="one element of each head's row"):
-            for row, table in ((W_ROW, w_mix), (B_ROW, b_mix)):
+        def load_out_scales():
+            for quadrant in range(4):
                 nc.sync.dma_start(
-                    out=head_rows[0:1, SLOT * row : SLOT * row + HEADS],
-                    in_=table[:, index : index + 1].rearrange("h o -> o h"),
+                    out=out_scales[32 * quadrant : 32 * quadrant + 4 * GROUPS, :].bitcast(I32),
+                    in_=W_out_scales[:, 4 * quadrant : 4 * quadrant + 4, :].bitcast(I32),
                 )
-        nc.sync.dma_start(
-            out=head_rows[0:1, SLOT * COEF_ROW : SLOT * COEF_ROW + HEADS], in_=decay_values.unsqueeze(0)
-        )
-        proj_bias = const.tile([P, GROUPS, PACK], BF16)
-        nc.sync.dma_start(
-            out=proj_bias[:], in_=b_proj.rearrange("h c -> (h c)").rearrange("(g q t) -> q g t", g=GROUPS, t=PACK)
-        )
-        x_sb = keep.tile([P, BATCH_TILES, DIM], BF16)
-        cache_tiles = {}
 
-        def load_x(i):
-            nc.sync.dma_start(out=x_sb[:, i, :], in_=x_rows[:, i, :])
+        out_tiles = {}
 
-        load_x(0)
-        load_x(1)
-        w_raw[(1, 0)] = load_half_group(1, 0)
-        load_x(2)
-        load_x(3)
-        w_raw[(1, 1)] = load_half_group(1, 1)
-        cache_tiles[0] = load_caches(0)
-        cache_tiles[1] = load_caches(1)
-        for half in range(HALVES):
-            w_raw[(2, half)] = load_half_group(2, half)
-        cache_tiles[2] = load_caches(2)
-        for half in range(HALVES):
-            w_raw[(3, half)] = load_half_group(3, half)
-        for quadrant in range(4):
-            nc.sync.dma_start(
-                out=out_scales[32 * quadrant : 32 * quadrant + 4 * GROUPS, :].bitcast(I32),
-                in_=W_out_scales[:, 4 * quadrant : 4 * quadrant + 4, :].bitcast(I32),
-            )
-        out_words = {}
-        out_bias = const.tile([P, DOUT], BF16)
-        for side in range(SIDES):
+        def load_out_words(side, g):
+            if g % 2 == 0:
+                out_tiles[(side, g // 2)] = ring.tile([P, 2, SIDE_COLS], U32, name="words", tag="weights", align_bytes=64)
+            words = out_tiles[(side, g // 2)]
             side_cols = slice(side * SIDE_COLS, (side + 1) * SIDE_COLS)
-            for g in range(GROUPS):
-                if g % 2 == 0:
-                    words = ring.tile([P, 2, SIDE_COLS], U32, name="words", tag="weights", align_bytes=64)
-                nc.sync.dma_start(
-                    out=words[:, g % 2, :].bitcast(I32),
-                    in_=W_out_words[g, :, side_cols, :].rearrange("q n t -> q (n t)").bitcast(I32),
-                )
-                for part in range(N_PER_SIDE):
-                    out_words[(side * N_PER_SIDE + part, g)] = words[:, g % 2, part * N_TILE : (part + 1) * N_TILE]
-                if (side, g) == (0, 1):
-                    cache_tiles[3] = load_caches(3)
+            nc.sync.dma_start(
+                out=words[:, g % 2, :].bitcast(I32),
+                in_=W_out_words[g, :, side_cols, :].rearrange("q n t -> q (n t)").bitcast(I32),
+            )
+            for part in range(N_PER_SIDE):
+                out_words[(side * N_PER_SIDE + part, g)] = words[:, g % 2, part * N_TILE : (part + 1) * N_TILE]
+
+        load_half_group(0, 0, split=2)
+        load_x(0)
+        load_half_group(0, 1)
+        load_half_group(1, 0)
+        load_x(1)
+        load_vectors()
+        load_half_group(1, 1)
+        for g in range(2, GROUPS):
+            for half in range(HALVES):
+                load_half_group(g, half)
+        load_caches(0)
+        load_caches(1)
+        load_out_scales()
+        load_out_words(0, 0)
+        load_caches(2)
+        load_out_words(0, 1)
+        load_caches(3)
+        load_out_words(0, 2)
+        load_out_words(0, 3)
         nc.sync.dma_start(out=out_bias[:], in_=b_out.partition_broadcast(P))
+        for g in range(GROUPS):
+            load_out_words(1, g)
 
         per_head = const.tile([P, 3, HEADS], F32)
         per_part = const.tile([P, 3, GROUPS], F32)
         shift = const.tile([P, GROUPS, PACK], F32)
 
-        def spread_heads():
-            spread = psum.tile([P, HEAD_COLS], F32, name="spread", tag="bank")
+        def spread_heads(number):
+            spread = bank(number, [P, HEAD_COLS], F32, "spread")
             nc.tensor.matmul(out=spread[:], lhsT=ones[:], rhs=head_rows[:], start=True, stop=True)
             nc.scalar.copy(out=per_head[:], in_=spread[:].rearrange("p (r s) -> p r s", s=SLOT)[:, 0:3, 0:HEADS])
             nc.gpsimd.tensor_scalar(
@@ -169,17 +196,18 @@ def tile_mixedrepeatheads_kernel(
 
         w_grouped, w_codes, w_scales = {}, {}, {}
 
-        def regroup(g, half, hh, all_scalar=False):
-            if hh == 0:
+        def regroup(g, half, hh, cc, copy):
+            if (g, half) not in w_grouped:
                 w_grouped[(g, half)] = triple.tile(
                     [P, 2, PACK, P, PACK], BF16, name="w_grouped", tag="w_grouped", align_bytes=64
                 )
             parts = slice(hh * HEAD_PARTS, (hh + 1) * HEAD_PARTS)
-            for cc, copy in ((0, nc.scalar.copy if all_scalar else nc.vector.tensor_copy), (1, nc.scalar.copy)):
-                copy(
-                    out=w_grouped[(g, half)][:, cc, :, parts, :].rearrange("q t m j -> q m j t"),
-                    in_=w_raw[(g, half)][:, hh, cc].rearrange("q j (m t) -> q m j t", t=PACK),
-                )
+            copy(
+                out=w_grouped[(g, half)][:, cc, :, parts, :].rearrange("q t m j -> q m j t"),
+                in_=w_raw[(g, half)][:, hh, cc].rearrange("q j (m t) -> q m j t", t=PACK),
+            )
+
+        by_vector, by_scalar = nc.vector.tensor_copy, nc.scalar.copy
 
         def quantise_weights(g, half):
             if half == 0:
@@ -192,90 +220,96 @@ def tile_mixedrepeatheads_kernel(
                 in_=w_grouped[(g, half)][:].rearrange("q c t m j -> q (c t m j)"),
             )
 
-        x_codes = keep.tile([P, BATCH_TILES, PASSES, P], U32, align_bytes=64)
-        x_scales = keep.tile([P, BATCH_TILES, PASSES, P], U8, align_bytes=64)
-        x_grouped = {}
+        x_codes = keep.tile([P, PASSES, BATCH], U32, align_bytes=64)
+        x_scales = keep.tile([P, PASSES, BATCH], U8, align_bytes=64)
+        x_grouped, x_turned = {}, {}
 
-        def turn_x(i):
-            x_words = x_sb[:, i, :].bitcast(F32)
-            x_grouped[i] = triple.tile([P, PASSES, P, PACK], BF16, name="x_grouped", tag="x_grouped", align_bytes=64)
-            for half in range(HALVES):
-                x_t = psum.tile([P, 2, 2, P], F32, name="x_t", tag="bank")
-                for cc in range(2):
-                    first = WORDS * (2 * half + cc)
-                    for u in range(2):
-                        nc.tensor.transpose(x_t[:, cc, u, :], x_words[:, first + u : first + WORDS : 2], ident[:])
-                copy = nc.vector.tensor_copy if half == 1 and i > 1 else nc.scalar.copy
-                copy(
-                    out=x_grouped[i][:, 2 * half : 2 * half + 2].bitcast(F32),
-                    in_=x_t[:].rearrange("q c u p -> q c p u"),
-                )
+        def turn_x(c, r, number):
+            x_turned[(c, r)] = bank(number, [P, 2, 2, P], F32, "x_turned")
+            for ii in range(2):
+                x_words = x_sb[:, 2 * r + ii, :].bitcast(F32)
+                for u in range(2):
+                    nc.tensor.transpose(
+                        x_turned[(c, r)][:, ii, u, :], x_words[:, WORDS * c + u : WORDS * (c + 1) : 2], ident[:]
+                    )
 
-        def quantise_x(i):
-            nc.vector.quantize_mx(
-                out=x_codes[:, i].rearrange("q c p -> q (c p)").bitcast(FP8X4),
-                scales=x_scales[:, i].rearrange("q c p -> q (c p)"),
-                in_=x_grouped[i][:].rearrange("q c p t -> q (c p t)"),
+        def group_x(c, r, copy):
+            if c not in x_grouped:
+                x_grouped[c] = pair.tile([P, BATCH, PACK], BF16, name="x_grouped", tag="x_grouped", align_bytes=64)
+            copy(
+                out=x_grouped[c][:, r * PAIR : (r + 1) * PAIR, :].rearrange("q p t -> q (p t)").bitcast(F32)
+                .rearrange("q (i p u) -> q i p u", i=2, u=2),
+                in_=x_turned[(c, r)][:].rearrange("q i u p -> q i p u"),
             )
 
-        rest, hid_grouped, proj = {}, {}, {}
+        def quantise_x(c):
+            nc.vector.quantize_mx(
+                out=x_codes[:, c, :].bitcast(FP8X4), scales=x_scales[:, c, :],
+                in_=x_grouped[c][:].rearrange("q p t -> q (p t)"),
+            )
+
+        def keep_busy(number, columns):
+            idle = bank(number, [P, N_TILE], F32, "idle")
+            for step in range(2):
+                nc.tensor.matmul(out=idle[:], lhsT=ones[:], rhs=columns, start=True, stop=True)
+
+        proj, mixed, cache_turned, hid_grouped = {}, {}, {}, {}
         hid_codes = keep.tile([P, GROUPS, BATCH], U32, align_bytes=64)
         hid_scales = keep.tile([P, GROUPS, BATCH], U8, align_bytes=64)
 
-        cache_t = {}
-
-        def turn_caches(g, step):
-            if step == 1:
-                rest[g] = triple.tile([P, PACK, BATCH_TILES, P], F32, name="rest", tag="rest")
-            for u in range(2):
-                if step == 0:
-                    cache_t[(g, u)] = psum.tile([P, BATCH_TILES, P], F32, name="cache_t", tag="bank")
-                    for i in range(BATCH_TILES):
-                        cache_words = cache_tiles[g][:, i].rearrange("p h n -> p (h n)").bitcast(F32)
-                        nc.tensor.transpose(cache_t[(g, u)][:, i, :], cache_words[:, u:WORDS:2], ident[:])
-                else:
-                    halves = cache_t[(g, u)][:].bitcast(BF16).rearrange("q i (p e) -> q i p e", e=2)
-                    for e in range(2):
-                        t = 2 * u + e
-                        nc.scalar.activation(
-                            out=rest[g][:, t], in_=halves[:, :, :, e], func=ACT.Identity,
-                            scale=per_part[:, COEF_ROW, g : g + 1], bias=shift[:, g, t : t + 1],
-                        )
-
-        def project(g, i):
-            proj[(g, i)] = psum.tile([P, PACK, P], F32, name="proj", tag="bank")
+        def project(g, c, first_bank):
             for t in range(PACK):
-                for c in range(PASSES):
-                    nc.tensor.matmul_mx(
-                        out=proj[(g, i)][:, t, :],
-                        lhsT=w_codes[g][:, c, t, :].bitcast(FP8X4), lhsT_scale=w_scales[g][:, c, t, :],
-                        rhs=x_codes[:, i, c, :].bitcast(FP8X4), rhs_scale=x_scales[:, i, c, :],
-                        start=(c == 0), stop=(c == PASSES - 1),
+                if c == 0:
+                    proj[(g, t)] = bank(first_bank + t, [P, BATCH], F32, "proj")
+                nc.tensor.matmul_mx(
+                    out=proj[(g, t)][:],
+                    lhsT=w_codes[g][:, c, t, :].bitcast(FP8X4), lhsT_scale=w_scales[g][:, c, t, :],
+                    rhs=x_codes[:, c, :].bitcast(FP8X4), rhs_scale=x_scales[:, c, :],
+                    start=(c == 0), stop=(c == PASSES - 1),
+                )
+
+        def take(g, t):
+            if t == 0:
+                mixed[g] = quad.tile([P, PACK, BATCH], F32, name="mixed", tag="mixed")
+            nc.scalar.activation(
+                out=mixed[g][:, t, :], in_=proj[(g, t)][:], func=ACT.Identity,
+                scale=per_part[:, W_ROW, g : g + 1], bias=shift[:, g, t : t + 1],
+            )
+
+        def turn_caches(g, r, number):
+            cache_turned[(g, r)] = bank(number, [P, PACK, PAIR], BF16, "cache_turned")
+            for ii in range(2):
+                features = cache_tiles[g][:, 2 * r + ii].rearrange("p h n -> p (h n)")
+                for t in range(PACK):
+                    nc.tensor.transpose(
+                        cache_turned[(g, r)][:, t, ii * P : (ii + 1) * P], features[:, t:K_PASS:PACK], ident_bf[:]
                     )
 
-        def mix(g, i):
-            if i == 0:
-                hid_grouped[g] = pair.tile(
-                    [P, BATCH_TILES, P, PACK], BF16, name="hid_grouped", tag="hid_grouped", align_bytes=64
-                )
+        def mix(g, r):
+            if r == 0:
+                hid_grouped[g] = pair.tile([P, BATCH, PACK], BF16, name="hid_grouped", tag="hid_grouped", align_bytes=64)
+            cols = slice(r * PAIR, (r + 1) * PAIR)
             nc.vector.scalar_tensor_tensor(
-                out=hid_grouped[g][:, i],
-                in0=proj[(g, i)][:].rearrange("q t p -> q p t"), scalar=per_part[:, W_ROW, g : g + 1],
-                in1=rest[g][:, :, i, :].rearrange("q t p -> q p t"),
+                out=hid_grouped[g][:, cols, :],
+                in0=cache_turned[(g, r)][:].rearrange("q t p -> q p t"), scalar=per_part[:, COEF_ROW, g : g + 1],
+                in1=mixed[g][:, :, cols].rearrange("q t p -> q p t"),
                 op0=ALU.mult, op1=ALU.add,
             )
 
-        def quantise_hidden(g, tiles):
-            cols = slice(tiles.start * P, tiles.stop * P)
+        def quantise_hidden(g, cols=slice(0, BATCH)):
             nc.vector.quantize_mx(
                 out=hid_codes[:, g, cols].bitcast(FP8X4), scales=hid_scales[:, g, cols],
-                in_=hid_grouped[g][:, tiles].rearrange("q i p t -> q (i p t)"),
+                in_=hid_grouped[g][:, cols].rearrange("q p t -> q (p t)"),
             )
 
-        def second_product_pass(acc, n, i, g, cols=slice(0, N_TILE)):
+        accs = {}
+
+        def out_pass(n, i, g, number=None, cols=slice(0, N_TILE)):
+            if g == 0:
+                accs[(n, i)] = bank(number, [P, N_TILE], F32, "acc")
             out_cols = slice(n * N_TILE + cols.start, n * N_TILE + cols.stop)
             nc.tensor.matmul_mx(
-                out=acc[:, cols],
+                out=accs[(n, i)][:, cols],
                 lhsT=hid_codes[:, g, i * P : (i + 1) * P].bitcast(FP8X4),
                 lhsT_scale=hid_scales[:, g, i * P : (i + 1) * P],
                 rhs=out_words[(n, g)][:, cols].bitcast(FP8X4),
@@ -283,98 +317,130 @@ def tile_mixedrepeatheads_kernel(
                 start=(g == 0), stop=(g == GROUPS - 1),
             )
 
-        def finish(acc, n, i, cols=slice(0, N_TILE)):
+        def finish(n, i, cols=slice(0, N_TILE)):
             out_cols = slice(n * N_TILE + cols.start, n * N_TILE + cols.stop)
             result = store_pool.tile([P, N_TILE], F32, name="result")
-            nc.vector.tensor_tensor(out=result[:, cols], in0=acc[:, cols], in1=out_bias[:, out_cols], op=ALU.add)
+            nc.vector.tensor_tensor(
+                out=result[:, cols], in0=accs[(n, i)][:, cols], in1=out_bias[:, out_cols], op=ALU.add
+            )
             nc.sync.dma_start(out=out_rows[:, i, out_cols], in_=result[:, cols])
 
-        regroup(0, 0, 0)
-        regroup(0, 0, 1)
+        regroup(0, 0, 0, 0, by_vector)
+        regroup(0, 0, 0, 1, by_scalar)
+        regroup(0, 0, 1, 0, by_vector)
+        regroup(0, 0, 1, 1, by_scalar)
+        turn_x(0, 0, 4)
+        turn_x(1, 0, 5)
+        group_x(0, 0, by_scalar)
         quantise_weights(0, 0)
-        regroup(0, 1, 0)
-        spread_heads()
-        regroup(0, 1, 1)
-        turn_x(0)
-        quantise_weights(0, 1)
-        turn_x(1)
+        turn_x(0, 1, 6)
+        turn_x(1, 1, 7)
+        group_x(1, 0, by_scalar)
+        group_x(0, 1, by_vector)
+        group_x(1, 1, by_scalar)
+        keep_busy(3, x_sb[:, 0, 0:N_TILE])
         quantise_x(0)
-        regroup(1, 0, 0)
+        regroup(0, 1, 0, 0, by_vector)
+        regroup(0, 1, 0, 1, by_scalar)
         quantise_x(1)
-        regroup(1, 0, 1)
-        turn_x(2)
+        project(0, 0, 0)
+        regroup(0, 1, 1, 0, by_vector)
+        regroup(0, 1, 1, 1, by_scalar)
+        turn_x(2, 0, 4)
+        turn_x(3, 0, 5)
+        project(0, 1, 0)
+        regroup(1, 0, 0, 0, by_vector)
+        regroup(1, 0, 0, 1, by_scalar)
+        quantise_weights(0, 1)
+        regroup(1, 0, 1, 0, by_vector)
+        regroup(1, 0, 1, 1, by_scalar)
+        group_x(2, 0, by_scalar)
+        group_x(3, 0, by_vector)
+        turn_x(2, 1, 6)
+        turn_x(3, 1, 7)
         quantise_weights(1, 0)
-        project(0, 0)
-        turn_x(3)
-        project(0, 1)
+        group_x(2, 1, by_scalar)
+        group_x(3, 1, by_scalar)
         quantise_x(2)
-        regroup(1, 1, 0)
-        regroup(1, 1, 1)
+        spread_heads(5)
+        project(0, 2, 0)
         quantise_x(3)
-        quantise_weights(1, 1)
-        turn_caches(0, 0)
-        project(0, 2)
-        project(0, 3)
-        turn_caches(1, 0)
-        turn_caches(0, 1)
-        for i in range(BATCH_TILES):
-            mix(0, i)
-        for i in range(BATCH_TILES):
-            project(1, i)
-        turn_caches(2, 0)
-        regroup(2, 0, 0)
-        regroup(2, 0, 1)
-        regroup(2, 1, 0)
-        quantise_weights(2, 0)
-        regroup(2, 1, 1, all_scalar=True)
-        quantise_hidden(0, slice(0, BATCH_TILES))
-        quantise_weights(2, 1)
-        turn_caches(1, 1)
-        turn_caches(2, 1)
-        regroup(3, 0, 0)
-        regroup(3, 0, 1)
-        for i in range(BATCH_TILES):
-            mix(1, i)
-        for i in range(BATCH_TILES):
-            project(2, i)
-        mix(2, 0)
-        quantise_hidden(1, slice(0, BATCH_TILES))
-        for i in range(1, BATCH_TILES):
-            mix(2, i)
-        quantise_weights(3, 0)
-        quantise_hidden(2, slice(0, BATCH_TILES))
-        regroup(3, 1, 0)
-        regroup(3, 1, 1, all_scalar=True)
-        quantise_weights(3, 1)
+        project(0, 3, 0)
 
-        accs = {}
-        early = [(0, i) for i in range(BATCH_TILES)] + [(1, 0), (1, 1)]
-        for g in range(GROUPS - 1):
-            if g == GROUPS - 2:
-                turn_caches(GROUPS - 1, 0)
-                turn_caches(GROUPS - 1, 1)
-            for n, i in early:
-                if g == 0:
-                    accs[(n, i)] = psum.tile([P, N_TILE], F32, name="acc", tag="bank")
-                second_product_pass(accs[(n, i)], n, i, g)
-        for i in range(BATCH_TILES):
-            project(GROUPS - 1, i)
-            mix(GROUPS - 1, i)
-            if i >= 1:
-                quantise_hidden(GROUPS - 1, slice(i - 1, i))
-        quantise_hidden(GROUPS - 1, slice(3, 4))
-        for i in range(BATCH_TILES):
-            for n in range(2):
-                if (n, i) in early:
-                    second_product_pass(accs[(n, i)], n, i, GROUPS - 1)
-                    finish(accs[(n, i)], n, i)
-        for n in range(1, OUT_TILES):
-            for i in range(BATCH_TILES):
-                if (n, i) not in early:
-                    width = N_TILE // 2 if (n, i) == (OUT_TILES - 1, BATCH_TILES - 1) else N_TILE
-                    for first in range(0, N_TILE, width):
-                        cols = slice(first, first + width)
-                        acc = psum.tile([P, N_TILE], F32, name="acc", tag="bank")
-                        for g in range(GROUPS):
-                            second_product_pass(acc, n, i, g, cols)
-                        finish(acc, n, i, cols)
+        regroup(1, 1, 0, 0, by_vector)
+        regroup(1, 1, 0, 1, by_scalar)
+        project(1, 0, 4)
+        project(1, 1, 4)
+        regroup(1, 1, 1, 0, by_vector)
+        regroup(1, 1, 1, 1, by_scalar)
+        take(0, 0)
+        take(0, 1)
+        steps = [(g, half) for g in range(1, GROUPS) for half in range(HALVES)]
+        for (last_g, last_half), (g, half) in zip(steps[1:], steps[2:]):
+            regroup(g, half, 0, 0, by_vector)
+            regroup(g, half, 0, 1, by_scalar)
+            quantise_weights(last_g, last_half)
+            for c in (2 * last_half, 2 * last_half + 1):
+                project(last_g, c, 4 * (last_g % 2))
+            regroup(g, half, 1, 0, by_vector)
+            regroup(g, half, 1, 1, by_scalar if (g, half) == (2, 1) else by_vector)
+            if half == 0:
+                take(g - 2, 2)
+                take(g - 2, 3)
+            else:
+                take(g - 1, 0)
+                take(g - 1, 1)
+        take(2, 2)
+        take(2, 3)
+
+        turn_caches(0, 0, 0)
+        turn_caches(0, 1, 1)
+        quantise_weights(3, 1)
+        mix(0, 0)
+        project(3, 2, 4)
+        turn_caches(1, 0, 2)
+        turn_caches(1, 1, 3)
+        project(3, 3, 4)
+        mix(0, 1)
+        for t in range(PACK):
+            take(3, t)
+        mix(1, 0)
+        quantise_hidden(0)
+        turn_caches(2, 0, 4)
+        turn_caches(2, 1, 5)
+        early = [(0, 0, 0), (0, 1, 1), (0, 2, 6), (0, 3, 7)]
+        for n, i, number in early:
+            out_pass(n, i, 0, number)
+        mix(1, 1)
+        mix(2, 0)
+        turn_caches(3, 0, 2)
+        turn_caches(3, 1, 3)
+        quantise_hidden(1)
+        mix(2, 1)
+        for n, i, number in early:
+            out_pass(n, i, 1)
+        mix(3, 0)
+        quantise_hidden(2)
+        mix(3, 1)
+        late = [(1, 0, 4), (1, 1, 5)]
+        for g in range(2):
+            for n, i, number in late:
+                out_pass(n, i, g, number)
+        for r in range(PAIRS):
+            quantise_hidden(3, slice(r * PAIR, (r + 1) * PAIR))
+        for n, i, number in early + late:
+            out_pass(n, i, 2)
+        for n, i in ((0, 0), (0, 1), (1, 0), (1, 1), (0, 2), (0, 3)):
+            out_pass(n, i, 3)
+            finish(n, i)
+        rest = [(n, i) for n in range(1, OUT_TILES) for i in range(BATCH_TILES) if (n, i) not in ((1, 0), (1, 1))]
+        numbers = (2, 3, 0, 4, 1, 5, 6, 7)
+        for step, (n, i) in enumerate(rest[:-1]):
+            for g in range(GROUPS):
+                out_pass(n, i, g, numbers[step % 8])
+            finish(n, i)
+        for step in range(2):
+            cols = slice(step * N_TILE // 2, (step + 1) * N_TILE // 2)
+            for g in range(GROUPS):
+                out_pass(OUT_TILES - 1, BATCH_TILES - 1, g, numbers[(len(rest) - 1 + step) % 8], cols)
+            finish(OUT_TILES - 1, BATCH_TILES - 1, cols)

@@ -76,7 +76,7 @@ def tile_mixedrepeatheads_kernel(
 
         w_raw, cache_tiles, out_words = {}, {}, {}
         proj_bias = const.tile([P, GROUPS, PACK], BF16)
-        x_sb = keep.tile([P, BATCH_TILES, DIM], BF16)
+        x_sb = {}
         out_bias = const.tile([P, DOUT], BF16)
 
         def load_half_group(g, half, split=1):
@@ -92,10 +92,11 @@ def tile_mixedrepeatheads_kernel(
             w_raw[(g, half)] = raw
 
         def load_x(half):
+            x_sb[half] = keep.tile([P, BATCH_TILES, DIM // HALVES], BF16, name="x_sb%d" % half)
             cols = slice(half * DIM // HALVES, (half + 1) * DIM // HALVES)
             for r in range(PAIRS):
                 tiles = slice(2 * r, 2 * r + 2)
-                nc.sync.dma_start(out=x_sb[:, tiles, cols], in_=x_rows[:, tiles, cols])
+                nc.sync.dma_start(out=x_sb[half][:, tiles, :], in_=x_rows[:, tiles, cols])
 
         def load_vectors():
             with nc.allow_non_contiguous_dma(reason="one element of each head's row"):
@@ -142,11 +143,11 @@ def tile_mixedrepeatheads_kernel(
                 out_words[(side * N_PER_SIDE + part, g)] = words[:, g % 2, part * N_TILE : (part + 1) * N_TILE]
 
         load_half_group(0, 0, split=2)
+        load_vectors()
         load_x(0)
         load_half_group(0, 1)
         load_half_group(1, 0)
         load_x(1)
-        load_vectors()
         load_half_group(1, 1)
         for g in range(2, GROUPS):
             for half in range(HALVES):
@@ -227,10 +228,11 @@ def tile_mixedrepeatheads_kernel(
         def turn_x(c, r, number):
             x_turned[(c, r)] = bank(number, [P, 2, 2, P], F32, "x_turned")
             for ii in range(2):
-                x_words = x_sb[:, 2 * r + ii, :].bitcast(F32)
+                x_words = x_sb[c // 2][:, 2 * r + ii, :].bitcast(F32)
+                first = WORDS * (c % 2)
                 for u in range(2):
                     nc.tensor.transpose(
-                        x_turned[(c, r)][:, ii, u, :], x_words[:, WORDS * c + u : WORDS * (c + 1) : 2], ident[:]
+                        x_turned[(c, r)][:, ii, u, :], x_words[:, first + u : first + WORDS : 2], ident[:]
                     )
 
         def group_x(c, r, copy):
@@ -329,6 +331,7 @@ def tile_mixedrepeatheads_kernel(
         regroup(0, 0, 0, 1, by_scalar)
         regroup(0, 0, 1, 0, by_vector)
         regroup(0, 0, 1, 1, by_scalar)
+        spread_heads(3)
         turn_x(0, 0, 4)
         turn_x(1, 0, 5)
         group_x(0, 0, by_scalar)
@@ -338,7 +341,7 @@ def tile_mixedrepeatheads_kernel(
         group_x(1, 0, by_scalar)
         group_x(0, 1, by_vector)
         group_x(1, 1, by_scalar)
-        keep_busy(3, x_sb[:, 0, 0:N_TILE])
+        keep_busy(3, x_sb[0][:, 0, 0:N_TILE])
         quantise_x(0)
         regroup(0, 1, 0, 0, by_vector)
         regroup(0, 1, 0, 1, by_scalar)
@@ -362,7 +365,6 @@ def tile_mixedrepeatheads_kernel(
         group_x(2, 1, by_scalar)
         group_x(3, 1, by_scalar)
         quantise_x(2)
-        spread_heads(5)
         project(0, 2, 0)
         quantise_x(3)
         project(0, 3, 0)

@@ -69,8 +69,6 @@ def tile_mixedrepeatheads_kernel(
         nc.scalar.activation(out=table_probe[:], in_=exponent[:, 0:1], func=ACT.Identity)
         ident = const.tile([P, P], F32)
         make_identity(nc, ident[:])
-        ident_bf = const.tile([P, P], BF16)
-        make_identity(nc, ident_bf[:])
         out_scales = keep.tile([P, DOUT], U8, align_bytes=64)
         nc.gpsimd.memset(out_scales[:].bitcast(I32), 0)
 
@@ -143,8 +141,8 @@ def tile_mixedrepeatheads_kernel(
                 out_words[(side * N_PER_SIDE + part, g)] = words[:, g % 2, part * N_TILE : (part + 1) * N_TILE]
 
         load_half_group(0, 0, split=2)
-        load_vectors()
         load_x(0)
+        load_vectors()
         load_half_group(0, 1)
         load_half_group(1, 0)
         load_x(1)
@@ -225,24 +223,28 @@ def tile_mixedrepeatheads_kernel(
         x_scales = keep.tile([P, PASSES, BATCH], U8, align_bytes=64)
         x_grouped, x_turned = {}, {}
 
-        def turn_x(c, r, number):
-            x_turned[(c, r)] = bank(number, [P, 2, 2, P], F32, "x_turned")
-            for ii in range(2):
-                x_words = x_sb[c // 2][:, 2 * r + ii, :].bitcast(F32)
-                first = WORDS * (c % 2)
+        def turn(tiles, first, number):
+            turned = bank(number, [P, 2, 2, P], F32, "turned")
+            for ii, words in enumerate(tiles):
                 for u in range(2):
-                    nc.tensor.transpose(
-                        x_turned[(c, r)][:, ii, u, :], x_words[:, first + u : first + WORDS : 2], ident[:]
-                    )
+                    nc.tensor.transpose(turned[:, ii, u, :], words[:, first + u : first + WORDS : 2], ident[:])
+            return turned
+
+        def interleave(grouped, turned, r, copy):
+            copy(
+                out=grouped[:, r * PAIR : (r + 1) * PAIR, :].rearrange("q p t -> q (p t)").bitcast(F32)
+                .rearrange("q (i p u) -> q i p u", i=2, u=2),
+                in_=turned[:].rearrange("q i u p -> q i p u"),
+            )
+
+        def turn_x(c, r, number):
+            tiles = [x_sb[c // 2][:, 2 * r + ii, :].bitcast(F32) for ii in range(2)]
+            x_turned[(c, r)] = turn(tiles, WORDS * (c % 2), number)
 
         def group_x(c, r, copy):
             if c not in x_grouped:
-                x_grouped[c] = pair.tile([P, BATCH, PACK], BF16, name="x_grouped", tag="x_grouped", align_bytes=64)
-            copy(
-                out=x_grouped[c][:, r * PAIR : (r + 1) * PAIR, :].rearrange("q p t -> q (p t)").bitcast(F32)
-                .rearrange("q (i p u) -> q i p u", i=2, u=2),
-                in_=x_turned[(c, r)][:].rearrange("q i u p -> q i p u"),
-            )
+                x_grouped[c] = pair.tile([P, BATCH, PACK], BF16, name="x_grouped", tag="grouped", align_bytes=64)
+            interleave(x_grouped[c], x_turned[(c, r)], r, copy)
 
         def quantise_x(c):
             nc.vector.quantize_mx(
@@ -255,7 +257,7 @@ def tile_mixedrepeatheads_kernel(
             for step in range(2):
                 nc.tensor.matmul(out=idle[:], lhsT=ones[:], rhs=columns, start=True, stop=True)
 
-        proj, mixed, cache_turned, hid_grouped = {}, {}, {}, {}
+        proj, mixed, cache_turned, cache_grouped, hid_grouped = {}, {}, {}, {}, {}
         hid_codes = keep.tile([P, GROUPS, BATCH], U32, align_bytes=64)
         hid_scales = keep.tile([P, GROUPS, BATCH], U8, align_bytes=64)
 
@@ -279,13 +281,13 @@ def tile_mixedrepeatheads_kernel(
             )
 
         def turn_caches(g, r, number):
-            cache_turned[(g, r)] = bank(number, [P, PACK, PAIR], BF16, "cache_turned")
-            for ii in range(2):
-                features = cache_tiles[g][:, 2 * r + ii].rearrange("p h n -> p (h n)")
-                for t in range(PACK):
-                    nc.tensor.transpose(
-                        cache_turned[(g, r)][:, t, ii * P : (ii + 1) * P], features[:, t:K_PASS:PACK], ident_bf[:]
-                    )
+            tiles = [cache_tiles[g][:, 2 * r + ii].rearrange("p h n -> p (h n)").bitcast(F32) for ii in range(2)]
+            cache_turned[(g, r)] = turn(tiles, 0, number)
+
+        def group_caches(g, r):
+            if r == 0:
+                cache_grouped[g] = pair.tile([P, BATCH, PACK], BF16, name="cache_grouped", tag="grouped", align_bytes=64)
+            interleave(cache_grouped[g], cache_turned[(g, r)], r, by_scalar)
 
         def mix(g, r):
             if r == 0:
@@ -293,7 +295,7 @@ def tile_mixedrepeatheads_kernel(
             cols = slice(r * PAIR, (r + 1) * PAIR)
             nc.vector.scalar_tensor_tensor(
                 out=hid_grouped[g][:, cols, :],
-                in0=cache_turned[(g, r)][:].rearrange("q t p -> q p t"), scalar=per_part[:, COEF_ROW, g : g + 1],
+                in0=cache_grouped[g][:, cols, :], scalar=per_part[:, COEF_ROW, g : g + 1],
                 in1=mixed[g][:, :, cols].rearrange("q t p -> q p t"),
                 op0=ALU.mult, op1=ALU.add,
             )
@@ -331,7 +333,6 @@ def tile_mixedrepeatheads_kernel(
         regroup(0, 0, 0, 1, by_scalar)
         regroup(0, 0, 1, 0, by_vector)
         regroup(0, 0, 1, 1, by_scalar)
-        spread_heads(3)
         turn_x(0, 0, 4)
         turn_x(1, 0, 5)
         group_x(0, 0, by_scalar)
@@ -341,6 +342,7 @@ def tile_mixedrepeatheads_kernel(
         group_x(1, 0, by_scalar)
         group_x(0, 1, by_vector)
         group_x(1, 1, by_scalar)
+        spread_heads(3)
         keep_busy(3, x_sb[0][:, 0, 0:N_TILE])
         quantise_x(0)
         regroup(0, 1, 0, 0, by_vector)
@@ -378,7 +380,7 @@ def tile_mixedrepeatheads_kernel(
         take(0, 0)
         take(0, 1)
         steps = [(g, half) for g in range(1, GROUPS) for half in range(HALVES)]
-        for (last_g, last_half), (g, half) in zip(steps[1:], steps[2:]):
+        for (last_g, last_half), (g, half) in zip(steps[1:-1], steps[2:-1]):
             regroup(g, half, 0, 0, by_vector)
             regroup(g, half, 0, 1, by_scalar)
             quantise_weights(last_g, last_half)
@@ -392,51 +394,68 @@ def tile_mixedrepeatheads_kernel(
             else:
                 take(g - 1, 0)
                 take(g - 1, 1)
-        take(2, 2)
-        take(2, 3)
-
+        regroup(3, 1, 0, 0, by_vector)
+        regroup(3, 1, 0, 1, by_scalar)
+        quantise_weights(3, 0)
+        project(3, 0, 4)
+        regroup(3, 1, 1, 0, by_vector)
+        regroup(3, 1, 1, 1, by_vector)
+        take(2, 0)
+        take(2, 1)
         turn_caches(0, 0, 0)
         turn_caches(0, 1, 1)
+        project(3, 1, 4)
+        take(2, 2)
+        group_caches(0, 0)
+        take(2, 3)
+        group_caches(0, 1)
+
         quantise_weights(3, 1)
         mix(0, 0)
         project(3, 2, 4)
         turn_caches(1, 0, 2)
         turn_caches(1, 1, 3)
+        group_caches(1, 0)
+        group_caches(1, 1)
         project(3, 3, 4)
         mix(0, 1)
         for t in range(PACK):
             take(3, t)
         mix(1, 0)
         quantise_hidden(0)
-        turn_caches(2, 0, 4)
-        turn_caches(2, 1, 5)
-        early = [(0, 0, 0), (0, 1, 1), (0, 2, 6), (0, 3, 7)]
+        turn_caches(2, 0, 0)
+        turn_caches(2, 1, 1)
+        early = [(0, 0, 2), (0, 1, 3), (0, 2, 4), (0, 3, 5)]
         for n, i, number in early:
             out_pass(n, i, 0, number)
         mix(1, 1)
-        mix(2, 0)
-        turn_caches(3, 0, 2)
-        turn_caches(3, 1, 3)
+        group_caches(2, 0)
+        group_caches(2, 1)
         quantise_hidden(1)
+        mix(2, 0)
+        turn_caches(3, 0, 6)
+        turn_caches(3, 1, 7)
         mix(2, 1)
         for n, i, number in early:
             out_pass(n, i, 1)
-        mix(3, 0)
-        quantise_hidden(2)
-        mix(3, 1)
-        late = [(1, 0, 4), (1, 1, 5)]
+        group_caches(3, 0)
+        group_caches(3, 1)
+        late = [(1, 0, 0), (1, 1, 1), (1, 2, 6), (1, 3, 7)]
         for g in range(2):
             for n, i, number in late:
                 out_pass(n, i, g, number)
-        for r in range(PAIRS):
-            quantise_hidden(3, slice(r * PAIR, (r + 1) * PAIR))
+        mix(3, 0)
+        quantise_hidden(2)
+        mix(3, 1)
         for n, i, number in early + late:
             out_pass(n, i, 2)
-        for n, i in ((0, 0), (0, 1), (1, 0), (1, 1), (0, 2), (0, 3)):
+        for r in range(PAIRS):
+            quantise_hidden(3, slice(r * PAIR, (r + 1) * PAIR))
+        for n, i in ((0, 0), (0, 1), (1, 0), (1, 1), (0, 2), (0, 3), (1, 2), (1, 3)):
             out_pass(n, i, 3)
             finish(n, i)
-        rest = [(n, i) for n in range(1, OUT_TILES) for i in range(BATCH_TILES) if (n, i) not in ((1, 0), (1, 1))]
-        numbers = (2, 3, 0, 4, 1, 5, 6, 7)
+        rest = [(n, i) for n in range(2, OUT_TILES) for i in range(BATCH_TILES)]
+        numbers = (2, 3, 0, 1, 4, 5, 6, 7)
         for step, (n, i) in enumerate(rest[:-1]):
             for g in range(GROUPS):
                 out_pass(n, i, g, numbers[step % 8])

@@ -61,7 +61,7 @@ def tile_mixedrepeatheads_kernel(
 
         head_rows = const.tile([P, HEAD_COLS], BF16)
         nc.vector.memset(head_rows[:].bitcast(I32), 0)
-        exponent = const.tile([P, HEADS], F32)
+        exponent = const.tile([P, GROUPS], F32)
         nc.vector.memset(exponent[:], decay_root)
         ones = const.tile([P, P], BF16)
         nc.vector.memset(ones[:], 1.0)
@@ -163,35 +163,28 @@ def tile_mixedrepeatheads_kernel(
         for g in range(GROUPS):
             load_out_words(1, g)
 
-        per_head = const.tile([P, 3, HEADS], F32)
         per_part = const.tile([P, 3, GROUPS], F32)
+        coef = const.tile([P, GROUPS], F32)
         shift = const.tile([P, GROUPS, PACK], F32)
 
         def spread_heads(number):
             spread = bank(number, [P, HEAD_COLS], F32, "spread")
             nc.tensor.matmul(out=spread[:], lhsT=ones[:], rhs=head_rows[:], start=True, stop=True)
-            nc.scalar.copy(out=per_head[:], in_=spread[:].rearrange("p (r s) -> p r s", s=SLOT)[:, 0:3, 0:HEADS])
-            nc.gpsimd.tensor_scalar(
-                out=per_head[:, COEF_ROW, :], in0=per_head[:, COEF_ROW, :],
-                scalar1=0.9, scalar2=1.0, op0=ALU.max, op1=ALU.min,
-            )
-            nc.gpsimd.tensor_tensor(
-                out=per_head[:, COEF_ROW, :], in0=per_head[:, COEF_ROW, :], in1=exponent[:], op=ALU.pow
-            )
-            first_heads = slice(0, HEADS // 2)
-            nc.gpsimd.tensor_tensor(
-                out=per_head[:, COEF_ROW, first_heads], in0=per_head[:, COEF_ROW, first_heads],
-                in1=per_head[:, W_ROW, first_heads], op=ALU.mult,
-            )
+            heads = spread[:].rearrange("p (r s) -> p r s", s=SLOT)
             for hh in range(GROUP_HEADS):
                 parts = slice(hh * HEAD_PARTS, (hh + 1) * HEAD_PARTS)
-                nc.gpsimd.tensor_copy(out=per_part[parts], in_=per_head[parts, :, hh:HEADS:GROUP_HEADS])
+                nc.scalar.copy(out=per_part[parts], in_=heads[parts, 0:3, hh:HEADS:GROUP_HEADS])
             for g in range(GROUPS):
-                nc.gpsimd.tensor_scalar(
-                    out=shift[:, g, :], in0=proj_bias[:, g, :],
-                    scalar1=per_part[:, W_ROW, g : g + 1], scalar2=per_part[:, B_ROW, g : g + 1],
-                    op0=ALU.mult, op1=ALU.add,
+                nc.scalar.activation(
+                    out=shift[:, g, :], in_=proj_bias[:, g, :], func=ACT.Identity,
+                    scale=per_part[:, W_ROW, g : g + 1], bias=per_part[:, B_ROW, g : g + 1],
                 )
+            nc.gpsimd.tensor_scalar(
+                out=coef[:], in0=per_part[:, COEF_ROW, :], scalar1=0.9, scalar2=1.0, op0=ALU.max, op1=ALU.min
+            )
+            nc.gpsimd.tensor_tensor(out=coef[:], in0=coef[:], in1=exponent[:], op=ALU.pow)
+            first = slice(0, GROUPS // 2)
+            nc.gpsimd.tensor_tensor(out=coef[:, first], in0=coef[:, first], in1=per_part[:, W_ROW, first], op=ALU.mult)
 
         w_grouped, w_codes, w_scales = {}, {}, {}
 
@@ -295,7 +288,7 @@ def tile_mixedrepeatheads_kernel(
             cols = slice(r * PAIR, (r + 1) * PAIR)
             nc.vector.scalar_tensor_tensor(
                 out=hid_grouped[g][:, cols, :],
-                in0=cache_grouped[g][:, cols, :], scalar=per_part[:, COEF_ROW, g : g + 1],
+                in0=cache_grouped[g][:, cols, :], scalar=coef[:, g : g + 1],
                 in1=mixed[g][:, :, cols].rearrange("q t p -> q p t"),
                 op0=ALU.mult, op1=ALU.add,
             )

@@ -245,9 +245,9 @@ def tile_mixedrepeatheads_kernel(
                 in_=x_grouped[c][:].rearrange("q p t -> q (p t)"),
             )
 
-        def keep_busy(number, columns):
+        def keep_busy(passes, number, columns):
             idle = bank(number, [P, N_TILE], F32, "idle")
-            for step in range(2):
+            for step in range(passes):
                 nc.tensor.matmul(out=idle[:], lhsT=ones[:], rhs=columns, start=True, stop=True)
 
         proj, mixed, cache_turned, cache_grouped, hid_grouped = {}, {}, {}, {}, {}
@@ -335,8 +335,8 @@ def tile_mixedrepeatheads_kernel(
         group_x(1, 0, by_scalar)
         group_x(0, 1, by_vector)
         group_x(1, 1, by_scalar)
-        spread_heads(3)
-        keep_busy(3, x_sb[0][:, 0, 0:N_TILE])
+        spread_heads(2)
+        keep_busy(3, 3, x_sb[0][:, 0, 0:N_TILE])
         quantise_x(0)
         regroup(0, 1, 0, 0, by_vector)
         regroup(0, 1, 0, 1, by_scalar)
@@ -344,9 +344,9 @@ def tile_mixedrepeatheads_kernel(
         project(0, 0, 0)
         regroup(0, 1, 1, 0, by_vector)
         regroup(0, 1, 1, 1, by_scalar)
+        project(0, 1, 0)
         turn_x(2, 0, 4)
         turn_x(3, 0, 5)
-        project(0, 1, 0)
         regroup(1, 0, 0, 0, by_vector)
         regroup(1, 0, 0, 1, by_scalar)
         quantise_weights(0, 1)
@@ -356,6 +356,7 @@ def tile_mixedrepeatheads_kernel(
         group_x(3, 0, by_vector)
         turn_x(2, 1, 6)
         turn_x(3, 1, 7)
+        keep_busy(2, 4, x_sb[0][:, 2, 0:N_TILE])
         quantise_weights(1, 0)
         group_x(2, 1, by_scalar)
         group_x(3, 1, by_scalar)
@@ -405,9 +406,9 @@ def tile_mixedrepeatheads_kernel(
 
         quantise_weights(3, 1)
         mix(0, 0)
-        project(3, 2, 4)
         turn_caches(1, 0, 2)
         turn_caches(1, 1, 3)
+        project(3, 2, 4)
         group_caches(1, 0)
         group_caches(1, 1)
         project(3, 3, 4)

@@ -90,7 +90,7 @@ def tile_mixedrepeatheads_kernel(
             w_raw[(g, half)] = raw
 
         def load_x(half):
-            x_sb[half] = keep.tile([P, BATCH_TILES, DIM // HALVES], BF16, name="x_sb%d" % half)
+            x_sb[half] = pair.tile([P, BATCH_TILES, DIM // HALVES], BF16, name="x_half", tag="x_half")
             cols = slice(half * DIM // HALVES, (half + 1) * DIM // HALVES)
             for r in range(PAIRS):
                 tiles = slice(2 * r, 2 * r + 2)
@@ -216,12 +216,15 @@ def tile_mixedrepeatheads_kernel(
         x_scales = keep.tile([P, PASSES, BATCH], U8, align_bytes=64)
         x_grouped, x_turned = {}, {}
 
-        def turn(tiles, first, number):
+        def turn(tiles, number):
             turned = bank(number, [P, 2, 2, P], F32, "turned")
-            for ii, words in enumerate(tiles):
+            for ii, columns in enumerate(tiles):
                 for u in range(2):
-                    nc.tensor.transpose(turned[:, ii, u, :], words[:, first + u : first + WORDS : 2], ident[:])
+                    nc.tensor.transpose(turned[:, ii, u, :], columns[u], ident[:])
             return turned
+
+        def every_second(words, first):
+            return [words[:, first + u : first + WORDS : 2] for u in range(2)]
 
         def interleave(grouped, turned, r, copy):
             copy(
@@ -232,7 +235,7 @@ def tile_mixedrepeatheads_kernel(
 
         def turn_x(c, r, number):
             tiles = [x_sb[c // 2][:, 2 * r + ii, :].bitcast(F32) for ii in range(2)]
-            x_turned[(c, r)] = turn(tiles, WORDS * (c % 2), number)
+            x_turned[(c, r)] = turn([every_second(words, WORDS * (c % 2)) for words in tiles], number)
 
         def group_x(c, r, copy):
             if c not in x_grouped:
@@ -273,9 +276,22 @@ def tile_mixedrepeatheads_kernel(
                 scale=per_part[:, W_ROW, g : g + 1], bias=shift[:, g, t : t + 1],
             )
 
+        cache_sorted = {}
+
+        def sort_caches(g):
+            cache_sorted[g] = pair.tile([P, BATCH_TILES, 2, P], F32, name="cache_sorted", tag="x_half")
+            nc.scalar.copy(
+                out=cache_sorted[g][:],
+                in_=cache_tiles[g][:].rearrange("p i h n -> p i (h n)").bitcast(F32).rearrange("p i (w u) -> p i u w", u=2),
+            )
+
         def turn_caches(g, r, number):
-            tiles = [cache_tiles[g][:, 2 * r + ii].rearrange("p h n -> p (h n)").bitcast(F32) for ii in range(2)]
-            cache_turned[(g, r)] = turn(tiles, 0, number)
+            if g in cache_sorted:
+                tiles = [[cache_sorted[g][:, 2 * r + ii, u, :] for u in range(2)] for ii in range(2)]
+            else:
+                words = [cache_tiles[g][:, 2 * r + ii].rearrange("p h n -> p (h n)").bitcast(F32) for ii in range(2)]
+                tiles = [every_second(tile, 0) for tile in words]
+            cache_turned[(g, r)] = turn(tiles, number)
 
         def group_caches(g, r):
             if r == 0:
@@ -353,7 +369,7 @@ def tile_mixedrepeatheads_kernel(
         regroup(1, 0, 1, 0, by_vector)
         regroup(1, 0, 1, 1, by_scalar)
         group_x(2, 0, by_scalar)
-        group_x(3, 0, by_vector)
+        group_x(3, 0, by_scalar)
         turn_x(2, 1, 6)
         turn_x(3, 1, 7)
         keep_busy(2, 4, x_sb[0][:, 2, 0:N_TILE])
@@ -388,9 +404,9 @@ def tile_mixedrepeatheads_kernel(
             else:
                 take(g - 1, 0)
                 take(g - 1, 1)
+        quantise_weights(3, 0)
         regroup(3, 1, 0, 0, by_vector)
         regroup(3, 1, 0, 1, by_scalar)
-        quantise_weights(3, 0)
         project(3, 0, 4)
         regroup(3, 1, 1, 0, by_vector)
         regroup(3, 1, 1, 1, by_vector)
@@ -413,6 +429,7 @@ def tile_mixedrepeatheads_kernel(
         group_caches(1, 1)
         project(3, 3, 4)
         mix(0, 1)
+        sort_caches(2)
         for t in range(PACK):
             take(3, t)
         mix(1, 0)

from contextlib import ExitStack

import concourse.mybir as mybir
from concourse.masks import make_identity

F32 = mybir.dt.float32
BF16 = mybir.dt.bfloat16
U32 = mybir.dt.uint32
U8 = mybir.dt.uint8
I32 = mybir.dt.int32
FP8X4 = mybir.dt.float8_e4m3fn_x4
ALU = mybir.AluOpType
ACT = mybir.ActivationFunctionType

P = 128
PACK = 4
K_PASS = P * PACK
BATCH, DIM, HID, HEADS, DOUT = 512, 2048, 256, 8, 2048
BATCH_TILES = BATCH // P
PAIR = 2 * P
PAIRS = BATCH // PAIR
PASSES = DIM // K_PASS
HALVES = 2
GROUPS = HEADS * HID // K_PASS
GROUP_HEADS = HEADS // GROUPS
HEAD_PARTS = HID // PACK
N_TILE = 512
OUT_TILES = DOUT // N_TILE
SIDES = 2
SIDE_COLS = DOUT // SIDES
N_PER_SIDE = SIDE_COLS // N_TILE
WORDS = K_PASS // 2
SLOT = 16
HEAD_COLS = 64
W_ROW, B_ROW, COEF_ROW = 0, 1, 2

FLOPS = 2 * BATCH * DIM * HEADS * HID + 2 * BATCH * HEADS * HID * DOUT


def tile_mixedrepeatheads_kernel(
    tc, x, index, W_proj, b_proj, W_out_words, W_out_scales, b_out, w_mix, b_mix, decay_values, caches, out
):
    nc = tc.nc
    decay_root = 1.0 / (w_mix.shape[1] // 512)
    x_rows = x.rearrange("(p i) k -> p i k", i=BATCH_TILES)
    out_rows = out.rearrange("(p i) n -> p i n", i=BATCH_TILES)

    with ExitStack() as ctx:
        ctx.enter_context(tc.manual_schedule())
        const = ctx.enter_context(tc.tile_pool(name="const", bufs=1))
        keep = ctx.enter_context(tc.tile_pool(name="keep", bufs=1))
        ring = ctx.enter_context(tc.tile_pool(name="ring", bufs=GROUPS * HALVES))
        pair = ctx.enter_context(tc.tile_pool(name="pair", bufs=2))
        triple = ctx.enter_context(tc.tile_pool(name="triple", bufs=3))
        quad = ctx.enter_context(tc.tile_pool(name="quad", bufs=GROUPS))
        store_pool = ctx.enter_context(tc.tile_pool(name="store", bufs=8))
        psum = ctx.enter_context(tc.psum_pool(name="psum", bufs=1))

        def bank(number, shape, dtype, name):
            return psum.tile(shape, dtype, name=name, tag="bank%d" % number)

        head_rows = const.tile([P, HEAD_COLS], BF16)
        nc.vector.memset(head_rows[:].bitcast(I32), 0)
        exponent = const.tile([P, GROUPS], F32)
        nc.vector.memset(exponent[:], decay_root)
        ones = const.tile([P, P], BF16)
        nc.vector.memset(ones[:], 1.0)
        table_probe = const.tile([P, 1], F32)
        nc.scalar.activation(out=table_probe[:], in_=exponent[:, 0:1], func=ACT.Identity)
        ident = const.tile([P, P], F32)
        make_identity(nc, ident[:])
        out_scales = keep.tile([P, DOUT], U8, align_bytes=64)
        nc.gpsimd.memset(out_scales[:].bitcast(I32), 0)

        w_raw, cache_tiles, out_words = {}, {}, {}
        proj_bias = const.tile([P, GROUPS, PACK], BF16)
        x_sb = {}
        out_bias = const.tile([P, DOUT], BF16)

        def load_half_group(g, half, split=1):
            raw = ring.tile([P, GROUP_HEADS, 2, PACK, HID], BF16, name="raw", tag="weights", align_bytes=64)
            for hh in range(GROUP_HEADS):
                by_pass = W_proj[GROUP_HEADS * g + hh].rearrange("(c q j) n -> q c j n", c=PASSES, j=PACK)
                for part in range(split):
                    passes = slice(part * 2 // split, (part + 1) * 2 // split)
                    nc.sync.dma_start(
                        out=raw[:, hh, passes],
                        in_=by_pass[:, 2 * half + passes.start : 2 * half + passes.stop],
                    )
            w_raw[(g, half)] = raw

        def load_x(half):
            x_sb[half] = pair.tile([P, BATCH_TILES, DIM // HALVES], BF16, name="x_half", tag="x_half")
            cols = slice(half * DIM // HALVES, (half + 1) * DIM // HALVES)
            for r in range(PAIRS):
                tiles = slice(2 * r, 2 * r + 2)
                nc.sync.dma_start(out=x_sb[half][:, tiles, :], in_=x_rows[:, tiles, cols])

        def load_vectors():
            with nc.allow_non_contiguous_dma(reason="one element of each head's row"):
                for row, table in ((W_ROW, w_mix), (B_ROW, b_mix)):
                    nc.sync.dma_start(
                        out=head_rows[0:1, SLOT * row : SLOT * row + HEADS],
                        in_=table[:, index : index + 1].rearrange("h o -> o h"),
                    )
            nc.sync.dma_start(
                out=head_rows[0:1, SLOT * COEF_ROW : SLOT * COEF_ROW + HEADS], in_=decay_values.unsqueeze(0)
            )
            nc.sync.dma_start(
                out=proj_bias[:],
                in_=b_proj.rearrange("h c -> (h c)").rearrange("(g q t) -> q g t", g=GROUPS, t=PACK),
            )

        def load_caches(g):
            cache_tiles[g] = keep.tile([P, BATCH_TILES, GROUP_HEADS, HID], BF16, name="cache_sb%d" % g)
            for hh in range(GROUP_HEADS):
                nc.sync.dma_start(
                    out=cache_tiles[g][:, :, hh, :],
                    in_=caches[GROUP_HEADS * g + hh].rearrange("(p i) n -> p i n", i=BATCH_TILES),
                )

        def load_out_scales():
            for quadrant in range(4):
                nc.sync.dma_start(
                    out=out_scales[32 * quadrant : 32 * quadrant + 4 * GROUPS, :].bitcast(I32),
                    in_=W_out_scales[:, 4 * quadrant : 4 * quadrant + 4, :].bitcast(I32),
                )

        out_tiles = {}

        def load_out_words(side, g):
            if g % 2 == 0:
                out_tiles[(side, g // 2)] = ring.tile([P, 2, SIDE_COLS], U32, name="words", tag="weights", align_bytes=64)
            words = out_tiles[(side, g // 2)]
            side_cols = slice(side * SIDE_COLS, (side + 1) * SIDE_COLS)
            nc.sync.dma_start(
                out=words[:, g % 2, :].bitcast(I32),
                in_=W_out_words[g, :, side_cols, :].rearrange("q n t -> q (n t)").bitcast(I32),
            )
            for part in range(N_PER_SIDE):
                out_words[(side * N_PER_SIDE + part, g)] = words[:, g % 2, part * N_TILE : (part + 1) * N_TILE]

        load_half_group(0, 0, split=2)
        load_x(0)
        load_vectors()
        load_half_group(0, 1)
        load_half_group(1, 0)
        load_x(1)
        load_half_group(1, 1)
        for g in range(2, GROUPS):
            for half in range(HALVES):
                load_half_group(g, half)
        load_caches(0)
        load_caches(1)
        load_out_scales()
        load_out_words(0, 0)
        load_caches(2)
        load_out_words(0, 1)
        load_caches(3)
        load_out_words(0, 2)
        load_out_words(0, 3)
        nc.sync.dma_start(out=out_bias[:], in_=b_out.partition_broadcast(P))
        for g in range(GROUPS):
            load_out_words(1, g)

        per_part = const.tile([P, 3, GROUPS], F32)
        coef = const.tile([P, GROUPS], F32)
        shift = const.tile([P, GROUPS, PACK], F32)

        def spread_heads(number):
            spread = bank(number, [P, HEAD_COLS], F32, "spread")
            nc.tensor.matmul(out=spread[:], lhsT=ones[:], rhs=head_rows[:], start=True, stop=True)
            heads = spread[:].rearrange("p (r s) -> p r s", s=SLOT)
            for hh in range(GROUP_HEADS):
                parts = slice(hh * HEAD_PARTS, (hh + 1) * HEAD_PARTS)
                nc.scalar.copy(out=per_part[parts], in_=heads[parts, 0:3, hh:HEADS:GROUP_HEADS])
            for g in range(GROUPS):
                nc.scalar.activation(
                    out=shift[:, g, :], in_=proj_bias[:, g, :], func=ACT.Identity,
                    scale=per_part[:, W_ROW, g : g + 1], bias=per_part[:, B_ROW, g : g + 1],
                )
            nc.gpsimd.tensor_scalar(
                out=coef[:], in0=per_part[:, COEF_ROW, :], scalar1=0.9, scalar2=1.0, op0=ALU.max, op1=ALU.min
            )
            nc.gpsimd.tensor_tensor(out=coef[:], in0=coef[:], in1=exponent[:], op=ALU.pow)
            first = slice(0, GROUPS // 2)
            nc.gpsimd.tensor_tensor(out=coef[:, first], in0=coef[:, first], in1=per_part[:, W_ROW, first], op=ALU.mult)

        w_grouped, w_codes, w_scales = {}, {}, {}

        def regroup(g, half, hh, cc, copy):
            if (g, half) not in w_grouped:
                w_grouped[(g, half)] = triple.tile(
                    [P, 2, PACK, P, PACK], BF16, name="w_grouped", tag="w_grouped", align_bytes=64
                )
            parts = slice(hh * HEAD_PARTS, (hh + 1) * HEAD_PARTS)
            copy(
                out=w_grouped[(g, half)][:, cc, :, parts, :].rearrange("q t m j -> q m j t"),
                in_=w_raw[(g, half)][:, hh, cc].rearrange("q j (m t) -> q m j t", t=PACK),
            )

        by_vector, by_scalar = nc.vector.tensor_copy, nc.scalar.copy

        def quantise_weights(g, half):
            if half == 0:
                w_codes[g] = pair.tile([P, PASSES, PACK, P], U32, name="w_codes", tag="w_codes", align_bytes=64)
                w_scales[g] = pair.tile([P, PASSES, PACK, P], U8, name="w_scales", tag="w_scales", align_bytes=64)
            two = slice(2 * half, 2 * half + 2)
            nc.vector.quantize_mx(
                out=w_codes[g][:, two].rearrange("q c t m -> q (c t m)").bitcast(FP8X4),
                scales=w_scales[g][:, two].rearrange("q c t m -> q (c t m)"),
                in_=w_grouped[(g, half)][:].rearrange("q c t m j -> q (c t m j)"),
            )

        x_codes = keep.tile([P, PASSES, BATCH], U32, align_bytes=64)
        x_scales = keep.tile([P, PASSES, BATCH], U8, align_bytes=64)
        x_grouped, x_turned = {}, {}

        def turn(tiles, number):
            turned = bank(number, [P, 2, 2, P], F32, "turned")
            for ii, columns in enumerate(tiles):
                for u in range(2):
                    nc.tensor.transpose(turned[:, ii, u, :], columns[u], ident[:])
            return turned

        def every_second(words, first):
            return [words[:, first + u : first + WORDS : 2] for u in range(2)]

        def interleave(grouped, turned, r, copy):
            copy(
                out=grouped[:, r * PAIR : (r + 1) * PAIR, :].rearrange("q p t -> q (p t)").bitcast(F32)
                .rearrange("q (i p u) -> q i p u", i=2, u=2),
                in_=turned[:].rearrange("q i u p -> q i p u"),
            )

        def turn_x(c, r, number):
            tiles = [x_sb[c // 2][:, 2 * r + ii, :].bitcast(F32) for ii in range(2)]
            x_turned[(c, r)] = turn([every_second(words, WORDS * (c % 2)) for words in tiles], number)

        def group_x(c, r, copy):
            if c not in x_grouped:
                x_grouped[c] = pair.tile([P, BATCH, PACK], BF16, name="x_grouped", tag="grouped", align_bytes=64)
            interleave(x_grouped[c], x_turned[(c, r)], r, copy)

        def quantise_x(c):
            nc.vector.quantize_mx(
                out=x_codes[:, c, :].bitcast(FP8X4), scales=x_scales[:, c, :],
                in_=x_grouped[c][:].rearrange("q p t -> q (p t)"),
            )

        def keep_busy(passes, number, columns):
            idle = bank(number, [P, N_TILE], F32, "idle")
            for step in range(passes):
                nc.tensor.matmul(out=idle[:], lhsT=ones[:], rhs=columns, start=True, stop=True)

        proj, mixed, cache_turned, cache_grouped, hid_grouped = {}, {}, {}, {}, {}
        hid_codes = keep.tile([P, GROUPS, BATCH], U32, align_bytes=64)
        hid_scales = keep.tile([P, GROUPS, BATCH], U8, align_bytes=64)

        def project(g, c, first_bank):
            for t in range(PACK):
                if c == 0:
                    proj[(g, t)] = bank(first_bank + t, [P, BATCH], F32, "proj")
                nc.tensor.matmul_mx(
                    out=proj[(g, t)][:],
                    lhsT=w_codes[g][:, c, t, :].bitcast(FP8X4), lhsT_scale=w_scales[g][:, c, t, :],
                    rhs=x_codes[:, c, :].bitcast(FP8X4), rhs_scale=x_scales[:, c, :],
                    start=(c == 0), stop=(c == PASSES - 1),
                )

        def take(g, t):
            if t == 0:
                mixed[g] = quad.tile([P, PACK, BATCH], F32, name="mixed", tag="mixed")
            nc.scalar.activation(
                out=mixed[g][:, t, :], in_=proj[(g, t)][:], func=ACT.Identity,
                scale=per_part[:, W_ROW, g : g + 1], bias=shift[:, g, t : t + 1],
            )

        cache_sorted = {}

        def sort_caches(g):
            cache_sorted[g] = pair.tile([P, BATCH_TILES, 2, P], F32, name="cache_sorted", tag="x_half")
            nc.scalar.copy(
                out=cache_sorted[g][:],
                in_=cache_tiles[g][:].rearrange("p i h n -> p i (h n)").bitcast(F32).rearrange("p i (w u) -> p i u w", u=2),
            )

        def turn_caches(g, r, number):
            if g in cache_sorted:
                tiles = [[cache_sorted[g][:, 2 * r + ii, u, :] for u in range(2)] for ii in range(2)]
            else:
                words = [cache_tiles[g][:, 2 * r + ii].rearrange("p h n -> p (h n)").bitcast(F32) for ii in range(2)]
                tiles = [every_second(tile, 0) for tile in words]
            cache_turned[(g, r)] = turn(tiles, number)

        def group_caches(g, r):
            if r == 0:
                cache_grouped[g] = pair.tile([P, BATCH, PACK], BF16, name="cache_grouped", tag="grouped", align_bytes=64)
            interleave(cache_grouped[g], cache_turned[(g, r)], r, by_scalar)

        def mix(g, r):
            if r == 0:
                hid_grouped[g] = pair.tile([P, BATCH, PACK], BF16, name="hid_grouped", tag="hid_grouped", align_bytes=64)
            cols = slice(r * PAIR, (r + 1) * PAIR)
            nc.vector.scalar_tensor_tensor(
                out=hid_grouped[g][:, cols, :],
                in0=cache_grouped[g][:, cols, :], scalar=coef[:, g : g + 1],
                in1=mixed[g][:, :, cols].rearrange("q t p -> q p t"),
                op0=ALU.mult, op1=ALU.add,
            )

        def quantise_hidden(g, cols=slice(0, BATCH)):
            nc.vector.quantize_mx(
                out=hid_codes[:, g, cols].bitcast(FP8X4), scales=hid_scales[:, g, cols],
                in_=hid_grouped[g][:, cols].rearrange("q p t -> q (p t)"),
            )

        accs = {}

        def out_pass(n, i, g, number=None, cols=slice(0, N_TILE)):
            if g == 0:
                accs[(n, i)] = bank(number, [P, N_TILE], F32, "acc")
            out_cols = slice(n * N_TILE + cols.start, n * N_TILE + cols.stop)
            nc.tensor.matmul_mx(
                out=accs[(n, i)][:, cols],
                lhsT=hid_codes[:, g, i * P : (i + 1) * P].bitcast(FP8X4),
                lhsT_scale=hid_scales[:, g, i * P : (i + 1) * P],
                rhs=out_words[(n, g)][:, cols].bitcast(FP8X4),
                rhs_scale=out_scales[4 * g : P, out_cols],
                start=(g == 0), stop=(g == GROUPS - 1),
            )

        def finish(n, i, cols=slice(0, N_TILE)):
            out_cols = slice(n * N_TILE + cols.start, n * N_TILE + cols.stop)
            result = store_pool.tile([P, N_TILE], F32, name="result")
            nc.vector.tensor_tensor(
                out=result[:, cols], in0=accs[(n, i)][:, cols], in1=out_bias[:, out_cols], op=ALU.add
            )
            nc.sync.dma_start(out=out_rows[:, i, out_cols], in_=result[:, cols])

        regroup(0, 0, 0, 0, by_vector)
        regroup(0, 0, 0, 1, by_scalar)
        regroup(0, 0, 1, 0, by_vector)
        regroup(0, 0, 1, 1, by_scalar)
        turn_x(0, 0, 4)
        turn_x(1, 0, 5)
        group_x(0, 0, by_scalar)
        quantise_weights(0, 0)
        turn_x(0, 1, 6)
        turn_x(1, 1, 7)
        group_x(1, 0, by_scalar)
        group_x(0, 1, by_vector)
        group_x(1, 1, by_scalar)
        spread_heads(2)
        keep_busy(3, 3, x_sb[0][:, 0, 0:N_TILE])
        quantise_x(0)
        regroup(0, 1, 0, 0, by_vector)
        regroup(0, 1, 0, 1, by_scalar)
        quantise_x(1)
        project(0, 0, 0)
        regroup(0, 1, 1, 0, by_vector)
        regroup(0, 1, 1, 1, by_scalar)
        project(0, 1, 0)
        turn_x(2, 0, 4)
        turn_x(3, 0, 5)
        regroup(1, 0, 0, 0, by_vector)
        regroup(1, 0, 0, 1, by_scalar)
        quantise_weights(0, 1)
        regroup(1, 0, 1, 0, by_vector)
        regroup(1, 0, 1, 1, by_scalar)
        group_x(2, 0, by_scalar)
        group_x(3, 0, by_scalar)
        turn_x(2, 1, 6)
        turn_x(3, 1, 7)
        keep_busy(2, 4, x_sb[0][:, 2, 0:N_TILE])
        quantise_weights(1, 0)
        group_x(2, 1, by_scalar)
        group_x(3, 1, by_scalar)
        quantise_x(2)
        project(0, 2, 0)
        quantise_x(3)
        project(0, 3, 0)

        regroup(1, 1, 0, 0, by_vector)
        regroup(1, 1, 0, 1, by_scalar)
        project(1, 0, 4)
        project(1, 1, 4)
        regroup(1, 1, 1, 0, by_vector)
        regroup(1, 1, 1, 1, by_scalar)
        take(0, 0)
        take(0, 1)
        steps = [(g, half) for g in range(1, GROUPS) for half in range(HALVES)]
        for (last_g, last_half), (g, half) in zip(steps[1:-1], steps[2:-1]):
            regroup(g, half, 0, 0, by_vector)
            regroup(g, half, 0, 1, by_scalar)
            quantise_weights(last_g, last_half)
            for c in (2 * last_half, 2 * last_half + 1):
                project(last_g, c, 4 * (last_g % 2))
            regroup(g, half, 1, 0, by_vector)
            regroup(g, half, 1, 1, by_scalar if (g, half) == (2, 1) else by_vector)
            if half == 0:
                take(g - 2, 2)
                take(g - 2, 3)
            else:
                take(g - 1, 0)
                take(g - 1, 1)
        quantise_weights(3, 0)
        regroup(3, 1, 0, 0, by_vector)
        regroup(3, 1, 0, 1, by_scalar)
        project(3, 0, 4)
        regroup(3, 1, 1, 0, by_vector)
        regroup(3, 1, 1, 1, by_vector)
        take(2, 0)
        take(2, 1)
        turn_caches(0, 0, 0)
        turn_caches(0, 1, 1)
        project(3, 1, 4)
        take(2, 2)
        group_caches(0, 0)
        take(2, 3)
        group_caches(0, 1)

        quantise_weights(3, 1)
        mix(0, 0)
        turn_caches(1, 0, 2)
        turn_caches(1, 1, 3)
        project(3, 2, 4)
        group_caches(1, 0)
        group_caches(1, 1)
        project(3, 3, 4)
        mix(0, 1)
        sort_caches(2)
        for t in range(PACK):
            take(3, t)
        mix(1, 0)
        quantise_hidden(0)
        turn_caches(2, 0, 0)
        turn_caches(2, 1, 1)
        early = [(0, 0, 2), (0, 1, 3), (0, 2, 4), (0, 3, 5)]
        for n, i, number in early:
            out_pass(n, i, 0, number)
        mix(1, 1)
        group_caches(2, 0)
        group_caches(2, 1)
        quantise_hidden(1)
        mix(2, 0)
        turn_caches(3, 0, 6)
        turn_caches(3, 1, 7)
        mix(2, 1)
        for n, i, number in early:
            out_pass(n, i, 1)
        group_caches(3, 0)
        group_caches(3, 1)
        late = [(1, 0, 0), (1, 1, 1), (1, 2, 6), (1, 3, 7)]
        for g in range(2):
            for n, i, number in late:
                out_pass(n, i, g, number)
        mix(3, 0)
        quantise_hidden(2)
        mix(3, 1)
        for n, i, number in early + late:
            out_pass(n, i, 2)
        for r in range(PAIRS):
            quantise_hidden(3, slice(r * PAIR, (r + 1) * PAIR))
        for n, i in ((0, 0), (0, 1), (1, 0), (1, 1), (0, 2), (0, 3), (1, 2), (1, 3)):
            out_pass(n, i, 3)
            finish(n, i)
        rest = [(n, i) for n in range(2, OUT_TILES) for i in range(BATCH_TILES)]
        numbers = (2, 3, 0, 1, 4, 5, 6, 7)
        for step, (n, i) in enumerate(rest[:-1]):
            for g in range(GROUPS):
                out_pass(n, i, g, numbers[step % 8])
            finish(n, i)
        for step in range(2):
            cols = slice(step * N_TILE // 2, (step + 1) * N_TILE // 2)
            for g in range(GROUPS):
                out_pass(OUT_TILES - 1, BATCH_TILES - 1, g, numbers[(len(rest) - 1 + step) % 8], cols)
            finish(OUT_TILES - 1, BATCH_TILES - 1, cols)
